import numpy as np
import ml_dtypes


def mxq(x, axis, fmt="e4m3"):
    dtype, down = {"e4m3": (ml_dtypes.float8_e4m3fn, 7), "e5m2": (ml_dtypes.float8_e5m2, 14)}[fmt]
    v = np.moveaxis(np.asarray(x, np.float32).astype(ml_dtypes.bfloat16).astype(np.float64), axis, -1)
    blocks = v.reshape(v.shape[:-1] + (-1, 32))
    amax = np.abs(blocks).max(-1, keepdims=True)
    byte = np.maximum(np.where(amax > 0, np.frexp(amax)[1] - 1 + 127, 0) - down, 1)
    scale = np.exp2(byte - 127.0)
    codes = (blocks / scale).astype(np.float32).astype(dtype).astype(np.float64)
    return np.moveaxis((codes * scale).reshape(v.shape), -1, axis)


WIDE = False


def mx_kscale(k):
    if not WIDE:
        return np.ones(k)
    levels = np.array([10, -10, 5, -5, 0])
    a = np.random.permutation(np.resize(levels, k // 512 * 4)).reshape(k // 512, 4)
    idx = np.arange(k)
    return np.exp2(a[idx // 512, idx % 128 // 32])


BF16 = ml_dtypes.bfloat16


def bf(x):
    return np.asarray(x, np.float32).astype(BF16)


def f64(x):
    return np.asarray(x).astype(np.float64)


L, R, T, H, F = 4, 4, 1024, 1024, 512


def setup_inputs():
    s, t = mx_kscale(H), mx_kscale(F)
    return {"x": bf(np.random.standard_normal((R, T, H)) * s),
            "w_first": bf(np.random.standard_normal((R, H, F)) / np.sqrt(R * H) / s[:, None] * t),
            "w_second": bf(np.random.standard_normal((R, F, H)) / np.sqrt(R * F) / t[:, None])}


def reference(x, w_first, w_second):
    y = mxq(f64(x), 2, "e4m3") @ mxq(f64(w_first), 1, "e4m3")
    reduced = y.sum(0)
    z = mxq(reduced, 1, "e4m3")[None] @ mxq(f64(w_second), 1, "e4m3")
    total = z.sum(0)
    return np.broadcast_to(total[None], z.shape).copy()

@@ -1,0 +1,207 @@
+from contextlib import ExitStack
+
+import concourse.mybir as mybir
+from concourse.masks import make_identity
+
+FP8X4 = mybir.dt.float8_e4m3fn_x4
+BF16 = mybir.dt.bfloat16
+F32 = mybir.dt.float32
+U32 = mybir.dt.uint32
+U8 = mybir.dt.uint8
+
+P = 128
+R, T, H, F = 4, 1024, 1024, 512
+A = T // P
+FLOPS = 2 * R * T * H * F * 2
+
+VEC_GROUPS = 80
+
+
+def tile_multilayerallreduce_pa_t_kernel(tc, x, w_first, w_second, out):
+    nc = tc.nc
+    with ExitStack() as ctx:
+        const = ctx.enter_context(tc.tile_pool(name="const", bufs=1))
+        xraw = ctx.enter_context(tc.tile_pool(name="xraw", bufs=4))
+        big = ctx.enter_context(tc.tile_pool(name="big", bufs=8))
+        xgp = ctx.enter_context(tc.tile_pool(name="xgp", bufs=2))
+        wgp = ctx.enter_context(tc.tile_pool(name="wgp", bufs=3))
+        keep = ctx.enter_context(tc.tile_pool(name="keep", bufs=1))
+        red = ctx.enter_context(tc.tile_pool(name="red", bufs=2))
+        psum = ctx.enter_context(tc.psum_pool(name="psum", bufs=8))
+
+        ident = const.tile([P, P], F32, name="ident")
+        make_identity(nc, ident[:])
+
+        x_rows = [x[r].rearrange("(m a) h -> m a h", a=A) for r in range(R)]
+        out_rows = [out[r].rearrange("(m a) n -> m a n", a=A) for r in range(R)]
+
+        xr0 = []
+        for r in range(R):
+            t0 = xraw.tile([P, 4 * H], BF16, name="xr0_%d" % r, tag="xr")
+            nc.sync.dma_start(out=t0[:].rearrange("p (a h) -> p a h", a=4), in_=x_rows[r][:, 0:4, :])
+            xr0.append(t0)
+        w1r = []
+        for r in range(R):
+            t1 = big.tile([P, 4, 2 * F], BF16, name="w1r_%d" % r, tag="big")
+            nc.sync.dma_start(out=t1[:], in_=w_first[r].rearrange("(s p e) f -> p s (e f)", p=P, e=2))
+            w1r.append(t1)
+        w2r = []
+        for r in range(R):
+            t2 = big.tile([P, 4, H], BF16, name="w2r_%d" % r, tag="big")
+            nc.sync.dma_start(out=t2[:], in_=w_second[r].rearrange("(j p) n -> p j n", p=P))
+            w2r.append(t2)
+
+        w1c = keep.tile([P, 2 * R, F], U32, name="w1c", align_bytes=64)
+        w1s = keep.tile([P, 2 * R, F], U8, name="w1s", align_bytes=64)
+        w2c = keep.tile([P, R, H], U32, name="w2c", align_bytes=64)
+        w2s = keep.tile([P, R, H], U8, name="w2s", align_bytes=64)
+
+        def x_path(raw, a_lo, na, r, codes, scales, engines):
+            words = raw[:].bitcast(F32)
+            grouped = xgp.tile([P, 2 * na * P * 4], BF16, name="xg", tag="xg", align_bytes=64)
+            gview = grouped[:].bitcast(F32).rearrange("p (g a m u) -> p g a m u", g=2, a=na, u=2)
+            for a in range(na):
+                bank = psum.tile([P, 4, P], F32, name="xt", tag="ps")
+                for s in range(4):
+                    lo = (a_lo + a) * (H // 2) + s * P
+                    nc.tensor.transpose(bank[:, s, :], words[:, lo : lo + P], ident[:])
+                src = bank[:].rearrange("p (g u) m -> p g m u", g=2)
+                if engines[a] == "v":
+                    nc.vector.tensor_copy(out=gview[:, :, a, :, :], in_=src)
+                else:
+                    nc.scalar.copy(out=gview[:, :, a, :, :], in_=src)
+            nc.vector.quantize_mx(out=codes[:, r, :].bitcast(FP8X4), scales=scales[:, r, :], in_=grouped[:])
+
+        def w_unit(src, codes, scales):
+            grouped = wgp.tile([P, 4 * 512], BF16, name="wg", tag="wg", align_bytes=64)
+            dv = grouped[:].rearrange("p (c i t) -> p c t i", i=4, t=4)
+            sv = src.rearrange("p t (c i) -> p c t i", i=4)
+            nc.vector.tensor_copy(out=dv[:, 0:VEC_GROUPS, :, :], in_=sv[:, 0:VEC_GROUPS, :, :])
+            nc.scalar.copy(out=dv[:, VEC_GROUPS:P, :, :], in_=sv[:, VEC_GROUPS:P, :, :])
+            nc.vector.quantize_mx(out=codes.bitcast(FP8X4), scales=scales, in_=grouped[:])
+
+        def l1_pass(acc, j, r, g, codes, scales, n):
+            nc.tensor.matmul_mx(
+                out=acc,
+                lhsT=w1c[:, 2 * r + g, j * P : (j + 1) * P].bitcast(FP8X4),
+                lhsT_scale=w1s[:, 2 * r + g, j * P : (j + 1) * P],
+                rhs=codes[:, r, g * n : (g + 1) * n].bitcast(FP8X4),
+                rhs_scale=scales[:, r, g * n : (g + 1) * n],
+                start=(r == 0 and g == 0),
+                stop=(r == R - 1 and g == 1),
+            )
+
+        def reduce_stage(acc_slices):
+            rb = red.tile([P, 4, 256], BF16, name="rb", tag="rb")
+            for j in range(4):
+                nc.scalar.copy(out=rb[:, j, :], in_=acc_slices[j])
+            rg = red.tile([P, 4 * 256], BF16, name="rg", tag="rg", align_bytes=64)
+            nc.vector.tensor_copy(
+                out=rg[:].rearrange("p (c i t) -> p c t i", i=4, t=4),
+                in_=rb[:].rearrange("p t (c i) -> p c t i", i=4),
+            )
+            rc = red.tile([P, 256], U32, name="rc", tag="rc", align_bytes=64)
+            rs = red.tile([P, 256], U8, name="rs", tag="rs", align_bytes=64)
+            nc.vector.quantize_mx(out=rc[:].bitcast(FP8X4), scales=rs[:], in_=rg[:])
+            return rc, rs
+
+        def l2_pass(acc, rc, rs, al, half, r):
+            nc.tensor.matmul_mx(
+                out=acc,
+                lhsT=rc[:, al * P : (al + 1) * P].bitcast(FP8X4),
+                lhsT_scale=rs[:, al * P : (al + 1) * P],
+                rhs=w2c[:, r, half * 512 : (half + 1) * 512].bitcast(FP8X4),
+                rhs_scale=w2s[:, r, half * 512 : (half + 1) * 512],
+                start=(r == 0),
+                stop=(r == R - 1),
+            )
+
+        def store(c, ot, per_row):
+            if per_row:
+                for al in range(2):
+                    for r in range(R):
+                        nc.sync.dma_start(out=out_rows[r][:, 2 * c + al, :], in_=ot[:, al, :])
+            else:
+                for r in range(R):
+                    nc.sync.dma_start(out=out_rows[r][:, 2 * c : 2 * c + 2, :], in_=ot[:])
+
+        def l2_chunk(c, rc, rs, per_row):
+            ot = big.tile([P, 2, H], F32, name="ot", tag="big")
+            for al in range(2):
+                for half in range(2):
+                    acc = psum.tile([P, 512], F32, name="acc2", tag="ps")
+                    for r in range(R):
+                        l2_pass(acc[:], rc, rs, al, half, r)
+                    nc.scalar.copy(out=ot[:, al, half * 512 : (half + 1) * 512], in_=acc[:])
+            store(c, ot, per_row)
+
+        xc0 = keep.tile([P, R, 1024], U32, name="xc0", align_bytes=64)
+        xs0 = keep.tile([P, R, 1024], U8, name="xs0", align_bytes=64)
+        for r in range(R):
+            x_path(xr0[r], 0, 4, r, xc0, xs0, "sssv")
+
+        xr1 = []
+        for r in range(R):
+            t3 = xraw.tile([P, 4 * H], BF16, name="xr1_%d" % r, tag="xr")
+            xr1.append(t3)
+        for c in range(2):
+            for r in range(R):
+                nc.sync.dma_start(
+                    out=xr1[r][:, 2 * c * H : (2 * c + 2) * H].rearrange("p (a h) -> p a h", a=2),
+                    in_=x_rows[r][:, 4 + 2 * c : 6 + 2 * c, :],
+                )
+
+        acc1 = [psum.tile([P, 512], F32, name="acc1_%d" % j, tag="ps") for j in range(4)]
+        for r in range(R):
+            rows = w1r[r][:].rearrange("p s (e f) -> p (s e) f", e=2)
+            for g in range(2):
+                w_unit(rows[:, 4 * g : 4 * g + 4, :], w1c[:, 2 * r + g, :], w1s[:, 2 * r + g, :])
+            for g in range(2):
+                for j in range(4):
+                    l1_pass(acc1[j][:], j, r, g, xc0, xs0, 512)
+
+        red0 = reduce_stage([acc1[j][:, 0:256] for j in range(4)])
+        red1 = reduce_stage([acc1[j][:, 256:512] for j in range(4)])
+
+        acc2 = [psum.tile([P, 512], F32, name="acc2_%d" % i, tag="ps") for i in range(4)]
+        for r in range(R):
+            for half in range(2):
+                w_unit(
+                    w2r[r][:, :, half * 512 : (half + 1) * 512],
+                    w2c[:, r, half * 512 : (half + 1) * 512],
+                    w2s[:, r, half * 512 : (half + 1) * 512],
+                )
+            for al in range(2):
+                for half in range(2):
+                    l2_pass(acc2[2 * al + half][:], red0[0], red0[1], al, half, r)
+        ot0 = big.tile([P, 2, H], F32, name="ot", tag="big")
+        for al in range(2):
+            for half in range(2):
+                nc.scalar.copy(out=ot0[:, al, half * 512 : (half + 1) * 512], in_=acc2[2 * al + half][:])
+        store(0, ot0, False)
+
+        def x_chunk(c):
+            codes = keep.tile([P, R, 512], U32, name="xc_%d" % c, align_bytes=64)
+            scales = keep.tile([P, R, 512], U8, name="xs_%d" % c, align_bytes=64)
+            for r in range(R):
+                x_path(xr1[r], 2 * (c - 2), 2, r, codes, scales, "sv")
+            return codes, scales
+
+        def l1_chunk(codes, scales):
+            slices = []
+            for jj in range(2):
+                acc = psum.tile([P, 2, 256], F32, name="acc1c", tag="ps")
+                for i in range(2):
+                    for r in range(R):
+                        for g in range(2):
+                            l1_pass(acc[:, i, :], 2 * jj + i, r, g, codes, scales, 256)
+                    slices.append(acc[:, i, :])
+            return reduce_stage(slices)
+
+        q2 = x_chunk(2)
+        l2_chunk(1, red1[0], red1[1], False)
+        red2 = l1_chunk(q2[0], q2[1])
+        q3 = x_chunk(3)
+        l2_chunk(2, red2[0], red2[1], False)
+        red3 = l1_chunk(q3[0], q3[1])
+        l2_chunk(3, red3[0], red3[1], True)

@@ -14,12 +14,15 @@ R, T, H, F = 4, 1024, 1024, 512
 A = T // P
 FLOPS = 2 * R * T * H * F * 2
 
-VEC_GROUPS = 80
+PINNED = True
+VEC_GROUPS = 64
 
 
 def tile_multilayerallreduce_pa_t_kernel(tc, x, w_first, w_second, out):
     nc = tc.nc
     with ExitStack() as ctx:
+        if PINNED:
+            ctx.enter_context(tc.manual_schedule())
         const = ctx.enter_context(tc.tile_pool(name="const", bufs=1))
         xraw = ctx.enter_context(tc.tile_pool(name="xraw", bufs=4))
         big = ctx.enter_context(tc.tile_pool(name="big", bufs=8))
@@ -27,21 +30,17 @@ def tile_multilayerallreduce_pa_t_kernel(tc, x, w_first, w_second, out):
         wgp = ctx.enter_context(tc.tile_pool(name="wgp", bufs=3))
         keep = ctx.enter_context(tc.tile_pool(name="keep", bufs=1))
         red = ctx.enter_context(tc.tile_pool(name="red", bufs=2))
-        psum = ctx.enter_context(tc.psum_pool(name="psum", bufs=8))
-
-        ident = const.tile([P, P], F32, name="ident")
-        make_identity(nc, ident[:])
+        psum = ctx.enter_context(tc.psum_pool(name="psum", bufs=4))
 
         x_rows = [x[r].rearrange("(m a) h -> m a h", a=A) for r in range(R)]
         out_rows = [out[r].rearrange("(m a) n -> m a n", a=A) for r in range(R)]
 
         xr0 = []
+        w1r = []
         for r in range(R):
             t0 = xraw.tile([P, 4 * H], BF16, name="xr0_%d" % r, tag="xr")
             nc.sync.dma_start(out=t0[:].rearrange("p (a h) -> p a h", a=4), in_=x_rows[r][:, 0:4, :])
             xr0.append(t0)
-        w1r = []
-        for r in range(R):
             t1 = big.tile([P, 4, 2 * F], BF16, name="w1r_%d" % r, tag="big")
             nc.sync.dma_start(out=t1[:], in_=w_first[r].rearrange("(s p e) f -> p s (e f)", p=P, e=2))
             w1r.append(t1)
@@ -51,94 +50,84 @@ def tile_multilayerallreduce_pa_t_kernel(tc, x, w_first, w_second, out):
             nc.sync.dma_start(out=t2[:], in_=w_second[r].rearrange("(j p) n -> p j n", p=P))
             w2r.append(t2)
 
+        ident = const.tile([P, P], F32, name="ident")
+        make_identity(nc, ident[:])
+
         w1c = keep.tile([P, 2 * R, F], U32, name="w1c", align_bytes=64)
         w1s = keep.tile([P, 2 * R, F], U8, name="w1s", align_bytes=64)
         w2c = keep.tile([P, R, H], U32, name="w2c", align_bytes=64)
         w2s = keep.tile([P, R, H], U8, name="w2s", align_bytes=64)
 
-        def x_path(raw, a_lo, na, r, codes, scales, engines):
+        def copy_on(engine, dst, src):
+            if engine == "v":
+                nc.vector.tensor_copy(out=dst, in_=src)
+            else:
+                nc.scalar.copy(out=dst, in_=src)
+
+        def x_path(raw, a_lo, na, r, codes, scales, engines, tags):
             words = raw[:].bitcast(F32)
             grouped = xgp.tile([P, 2 * na * P * 4], BF16, name="xg", tag="xg", align_bytes=64)
             gview = grouped[:].bitcast(F32).rearrange("p (g a m u) -> p g a m u", g=2, a=na, u=2)
             for a in range(na):
-                bank = psum.tile([P, 4, P], F32, name="xt", tag="ps")
+                bank = psum.tile([P, 4, P], F32, name="xt", tag=tags[a])
                 for s in range(4):
                     lo = (a_lo + a) * (H // 2) + s * P
                     nc.tensor.transpose(bank[:, s, :], words[:, lo : lo + P], ident[:])
-                src = bank[:].rearrange("p (g u) m -> p g m u", g=2)
-                if engines[a] == "v":
-                    nc.vector.tensor_copy(out=gview[:, :, a, :, :], in_=src)
-                else:
-                    nc.scalar.copy(out=gview[:, :, a, :, :], in_=src)
+                copy_on(engines[a], gview[:, :, a, :, :], bank[:].rearrange("p (g u) m -> p g m u", g=2))
             nc.vector.quantize_mx(out=codes[:, r, :].bitcast(FP8X4), scales=scales[:, r, :], in_=grouped[:])
 
-        def w_unit(src, codes, scales):
+        def w_regroup(src):
             grouped = wgp.tile([P, 4 * 512], BF16, name="wg", tag="wg", align_bytes=64)
             dv = grouped[:].rearrange("p (c i t) -> p c t i", i=4, t=4)
             sv = src.rearrange("p t (c i) -> p c t i", i=4)
             nc.vector.tensor_copy(out=dv[:, 0:VEC_GROUPS, :, :], in_=sv[:, 0:VEC_GROUPS, :, :])
             nc.scalar.copy(out=dv[:, VEC_GROUPS:P, :, :], in_=sv[:, VEC_GROUPS:P, :, :])
+            return grouped
+
+        def w_quantise(grouped, codes, scales):
             nc.vector.quantize_mx(out=codes.bitcast(FP8X4), scales=scales, in_=grouped[:])
 
-        def l1_pass(acc, j, r, g, codes, scales, n):
+        def l1_pass(acc, j, r, g, codes, scales, lo, n):
             nc.tensor.matmul_mx(
                 out=acc,
                 lhsT=w1c[:, 2 * r + g, j * P : (j + 1) * P].bitcast(FP8X4),
                 lhsT_scale=w1s[:, 2 * r + g, j * P : (j + 1) * P],
-                rhs=codes[:, r, g * n : (g + 1) * n].bitcast(FP8X4),
-                rhs_scale=scales[:, r, g * n : (g + 1) * n],
+                rhs=codes[:, r, lo : lo + n].bitcast(FP8X4),
+                rhs_scale=scales[:, r, lo : lo + n],
                 start=(r == 0 and g == 0),
                 stop=(r == R - 1 and g == 1),
             )
 
-        def reduce_stage(acc_slices):
-            rb = red.tile([P, 4, 256], BF16, name="rb", tag="rb")
-            for j in range(4):
-                nc.scalar.copy(out=rb[:, j, :], in_=acc_slices[j])
-            rg = red.tile([P, 4 * 256], BF16, name="rg", tag="rg", align_bytes=64)
-            nc.vector.tensor_copy(
-                out=rg[:].rearrange("p (c i t) -> p c t i", i=4, t=4),
-                in_=rb[:].rearrange("p t (c i) -> p c t i", i=4),
-            )
-            rc = red.tile([P, 256], U32, name="rc", tag="rc", align_bytes=64)
-            rs = red.tile([P, 256], U8, name="rs", tag="rs", align_bytes=64)
-            nc.vector.quantize_mx(out=rc[:].bitcast(FP8X4), scales=rs[:], in_=rg[:])
-            return rc, rs
-
-        def l2_pass(acc, rc, rs, al, half, r):
+        def l2_pass(acc, rc, rs, lo, half, r):
             nc.tensor.matmul_mx(
                 out=acc,
-                lhsT=rc[:, al * P : (al + 1) * P].bitcast(FP8X4),
-                lhsT_scale=rs[:, al * P : (al + 1) * P],
+                lhsT=rc[:, lo : lo + P].bitcast(FP8X4),
+                lhsT_scale=rs[:, lo : lo + P],
                 rhs=w2c[:, r, half * 512 : (half + 1) * 512].bitcast(FP8X4),
                 rhs_scale=w2s[:, r, half * 512 : (half + 1) * 512],
                 start=(r == 0),
                 stop=(r == R - 1),
             )
 
-        def store(c, ot, per_row):
-            if per_row:
-                for al in range(2):
-                    for r in range(R):
-                        nc.sync.dma_start(out=out_rows[r][:, 2 * c + al, :], in_=ot[:, al, :])
-            else:
-                for r in range(R):
-                    nc.sync.dma_start(out=out_rows[r][:, 2 * c : 2 * c + 2, :], in_=ot[:])
-
-        def l2_chunk(c, rc, rs, per_row):
-            ot = big.tile([P, 2, H], F32, name="ot", tag="big")
-            for al in range(2):
-                for half in range(2):
-                    acc = psum.tile([P, 512], F32, name="acc2", tag="ps")
-                    for r in range(R):
-                        l2_pass(acc[:], rc, rs, al, half, r)
-                    nc.scalar.copy(out=ot[:, al, half * 512 : (half + 1) * 512], in_=acc[:])
-            store(c, ot, per_row)
-
         xc0 = keep.tile([P, R, 1024], U32, name="xc0", align_bytes=64)
         xs0 = keep.tile([P, R, 1024], U8, name="xs0", align_bytes=64)
+        acc1 = []
+
+        x_path(xr0[0], 0, 4, 0, xc0, xs0, "sssv", ["hi"] * 4)
         for r in range(R):
-            x_path(xr0[r], 0, 4, r, xc0, xs0, "sssv")
+            rows = w1r[r][:].rearrange("p s (e f) -> p (s e) f", e=2)
+            grouped = [w_regroup(rows[:, 4 * g : 4 * g + 4, :]) for g in range(2)]
+            for g in range(2):
+                w_quantise(grouped[g], w1c[:, 2 * r + g, :], w1s[:, 2 * r + g, :])
+            if r + 1 < R:
+                x_path(xr0[r + 1], 0, 4, r + 1, xc0, xs0, "sssv", ["hi"] * 4)
+            if r == 0:
+                for j in range(4):
+                    acc_j = psum.tile([P, 512], F32, name="acc1_%d" % j, tag="lo")
+                    acc1.append(acc_j)
+            for g in range(2):
+                for j in range(4):
+                    l1_pass(acc1[j][:], j, r, g, xc0, xs0, g * 512, 512)
 
         xr1 = []
         for r in range(R):
@@ -151,57 +140,101 @@ def tile_multilayerallreduce_pa_t_kernel(tc, x, w_first, w_second, out):
                     in_=x_rows[r][:, 4 + 2 * c : 6 + 2 * c, :],
                 )
 
-        acc1 = [psum.tile([P, 512], F32, name="acc1_%d" % j, tag="ps") for j in range(4)]
-        for r in range(R):
-            rows = w1r[r][:].rearrange("p s (e f) -> p (s e) f", e=2)
-            for g in range(2):
-                w_unit(rows[:, 4 * g : 4 * g + 4, :], w1c[:, 2 * r + g, :], w1s[:, 2 * r + g, :])
-            for g in range(2):
-                for j in range(4):
-                    l1_pass(acc1[j][:], j, r, g, xc0, xs0, 512)
+        units = [(r, half) for r in range(R) for half in range(2)]
 
-        red0 = reduce_stage([acc1[j][:, 0:256] for j in range(4)])
-        red1 = reduce_stage([acc1[j][:, 256:512] for j in range(4)])
+        def w2_regroup(u):
+            return w_regroup(w2r[units[u][0]][:, :, units[u][1] * 512 : (units[u][1] + 1) * 512])
 
-        acc2 = [psum.tile([P, 512], F32, name="acc2_%d" % i, tag="ps") for i in range(4)]
-        for r in range(R):
-            for half in range(2):
-                w_unit(
-                    w2r[r][:, :, half * 512 : (half + 1) * 512],
-                    w2c[:, r, half * 512 : (half + 1) * 512],
-                    w2s[:, r, half * 512 : (half + 1) * 512],
-                )
+        rb = [None, None]
+        redq = [None, None]
+        acc2 = [[], []]
+        done = [0, 0]
+        nxt = w2_regroup(0)
+        for u in range(8):
+            cur = nxt
+            if u + 1 < 8:
+                nxt = w2_regroup(u + 1)
+            r, half = units[u]
+            w_quantise(cur, w2c[:, r, half * 512 : (half + 1) * 512], w2s[:, r, half * 512 : (half + 1) * 512])
+            for c in range(2):
+                if u == 1 + c:
+                    rb_c = red.tile([P, 4, 256], BF16, name="rb", tag="rb")
+                    for j in range(4):
+                        nc.scalar.copy(out=rb_c[:, j, :], in_=acc1[j][:, c * 256 : (c + 1) * 256])
+                    rb[c] = rb_c
+                if u == 2 + c:
+                    rg = red.tile([P, 4 * 256], BF16, name="rg", tag="rg", align_bytes=64)
+                    nc.vector.tensor_copy(
+                        out=rg[:].rearrange("p (c i t) -> p c t i", i=4, t=4),
+                        in_=rb[c][:].rearrange("p t (c i) -> p c t i", i=4),
+                    )
+                    rc = red.tile([P, 256], U32, name="rc", tag="rc", align_bytes=64)
+                    rs = red.tile([P, 256], U8, name="rs", tag="rs", align_bytes=64)
+                    nc.vector.quantize_mx(out=rc[:].bitcast(FP8X4), scales=rs[:], in_=rg[:])
+                    redq[c] = (rc, rs)
+                    for i in range(4):
+                        acc_i = psum.tile([P, 512], F32, name="acc2_%d_%d" % (c, i), tag=("hi", "lo")[c])
+                        acc2[c].append(acc_i)
+            ranks_ready = (u + 1) // 2
+            for c in range(2):
+                if redq[c] is not None:
+                    for rr in range(done[c], ranks_ready):
+                        for al in range(2):
+                            for hh in range(2):
+                                l2_pass(acc2[c][2 * al + hh][:], redq[c][0], redq[c][1], al * P, hh, rr)
+                    done[c] = ranks_ready
+
+        for c in range(2):
+            ot = big.tile([P, 2, H], F32, name="ot", tag="big")
             for al in range(2):
-                for half in range(2):
-                    l2_pass(acc2[2 * al + half][:], red0[0], red0[1], al, half, r)
-        ot0 = big.tile([P, 2, H], F32, name="ot", tag="big")
-        for al in range(2):
-            for half in range(2):
-                nc.scalar.copy(out=ot0[:, al, half * 512 : (half + 1) * 512], in_=acc2[2 * al + half][:])
-        store(0, ot0, False)
+                for hh in range(2):
+                    copy_on("sv"[hh], ot[:, al, hh * 512 : (hh + 1) * 512], acc2[c][2 * al + hh][:])
+            for r in range(R):
+                nc.sync.dma_start(out=out_rows[r][:, 2 * c : 2 * c + 2, :], in_=ot[:])
+
+        banks = [0]
+
+        def next_tag():
+            banks[0] += 1
+            return ("hi", "lo")[((banks[0] - 1) // 4) % 2]
 
         def x_chunk(c):
             codes = keep.tile([P, R, 512], U32, name="xc_%d" % c, align_bytes=64)
             scales = keep.tile([P, R, 512], U8, name="xs_%d" % c, align_bytes=64)
             for r in range(R):
-                x_path(xr1[r], 2 * (c - 2), 2, r, codes, scales, "sv")
+                x_path(xr1[r], 2 * (c - 2), 2, r, codes, scales, ("ss", "sv")[r % 2], [next_tag(), next_tag()])
             return codes, scales
 
-        def l1_chunk(codes, scales):
-            slices = []
-            for jj in range(2):
-                acc = psum.tile([P, 2, 256], F32, name="acc1c", tag="ps")
-                for i in range(2):
-                    for r in range(R):
-                        for g in range(2):
-                            l1_pass(acc[:, i, :], 2 * jj + i, r, g, codes, scales, 256)
-                    slices.append(acc[:, i, :])
-            return reduce_stage(slices)
+        def l1_tile(q, al):
+            bank = psum.tile([P, 4, P], F32, name="acc1t", tag=next_tag())
+            for j in range(4):
+                for r in range(R):
+                    for g in range(2):
+                        l1_pass(bank[:, j, :], j, r, g, q[0], q[1], g * 256 + al * P, P)
+            rg = red.tile([P, 4 * P], BF16, name="rgt", tag="rgt", align_bytes=64)
+            nc.scalar.copy(out=rg[:].rearrange("p (m j) -> p m j", j=4), in_=bank[:].rearrange("p j m -> p m j"))
+            rc = red.tile([P, P], U32, name="rct", tag="rct", align_bytes=64)
+            rs = red.tile([P, P], U8, name="rst", tag="rst", align_bytes=64)
+            nc.vector.quantize_mx(out=rc[:].bitcast(FP8X4), scales=rs[:], in_=rg[:])
+            return rc, rs
+
+        def l2_tile(rq, ot, al):
+            for hh in range(2):
+                acc = psum.tile([P, 512], F32, name="acc2t", tag=next_tag())
+                for r in range(R):
+                    l2_pass(acc[:], rq[0], rq[1], 0, hh, r)
+                copy_on("sv"[hh], ot[:, al, hh * 512 : (hh + 1) * 512], acc[:])
 
         q2 = x_chunk(2)
-        l2_chunk(1, red1[0], red1[1], False)
-        red2 = l1_chunk(q2[0], q2[1])
         q3 = x_chunk(3)
-        l2_chunk(2, red2[0], red2[1], False)
-        red3 = l1_chunk(q3[0], q3[1])
-        l2_chunk(3, red3[0], red3[1], True)
+        for c, q in ((2, q2), (3, q3)):
+            rq = [l1_tile(q, al) for al in range(2)]
+            ot = big.tile([P, 2, H], F32, name="ot", tag="big")
+            for al in range(2):
+                l2_tile(rq[al], ot, al)
+                if c == 3:
+                    for r in range(R):
+                        nc.sync.dma_start(out=out_rows[r][:, 2 * c + al, :], in_=ot[:, al, :])
+            if c == 2:
+                for r in range(R):
+                    nc.sync.dma_start(out=out_rows[r][:, 2 * c : 2 * c + 2, :], in_=ot[:])

@@ -14,41 +14,68 @@ R, T, H, F = 4, 1024, 1024, 512
 A = T // P
 FLOPS = 2 * R * T * H * F * 2
 
-PINNED = True
-VEC_GROUPS = 64
+VG0 = 64
+VG1 = 64
+X1_ENG = "vsss"
+VG2 = 64
+VG3 = 64
+RB_ENG = "ssvv"
+H0_ENG = "svsv"
+H1_ENG = "svsv"
 
 
 def tile_multilayerallreduce_pa_t_kernel(tc, x, w_first, w_second, out):
     nc = tc.nc
     with ExitStack() as ctx:
-        if PINNED:
-            ctx.enter_context(tc.manual_schedule())
+        ctx.enter_context(tc.manual_schedule())
         const = ctx.enter_context(tc.tile_pool(name="const", bufs=1))
         xraw = ctx.enter_context(tc.tile_pool(name="xraw", bufs=4))
-        big = ctx.enter_context(tc.tile_pool(name="big", bufs=8))
+        big = ctx.enter_context(tc.tile_pool(name="big", bufs=4))
+        w2p = ctx.enter_context(tc.tile_pool(name="w2p", bufs=8))
         xgp = ctx.enter_context(tc.tile_pool(name="xgp", bufs=2))
         wgp = ctx.enter_context(tc.tile_pool(name="wgp", bufs=3))
         keep = ctx.enter_context(tc.tile_pool(name="keep", bufs=1))
         red = ctx.enter_context(tc.tile_pool(name="red", bufs=2))
         psum = ctx.enter_context(tc.psum_pool(name="psum", bufs=4))
 
-        x_rows = [x[r].rearrange("(m a) h -> m a h", a=A) for r in range(R)]
+        x_flat = [x[r].rearrange("(m a) h -> m (a h)", a=A) for r in range(R)]
         out_rows = [out[r].rearrange("(m a) n -> m a n", a=A) for r in range(R)]
+        w1_view = [w_first[r].rearrange("(s p e) f -> p s (e f)", p=P, e=2) for r in range(R)]
+        w2_view = [w_second[r].rearrange("(j p) n -> p j n", p=P) for r in range(R)]
 
         xr0 = []
         w1r = []
         for r in range(R):
             t0 = xraw.tile([P, 4 * H], BF16, name="xr0_%d" % r, tag="xr")
-            nc.sync.dma_start(out=t0[:].rearrange("p (a h) -> p a h", a=4), in_=x_rows[r][:, 0:4, :])
             xr0.append(t0)
             t1 = big.tile([P, 4, 2 * F], BF16, name="w1r_%d" % r, tag="big")
-            nc.sync.dma_start(out=t1[:], in_=w_first[r].rearrange("(s p e) f -> p s (e f)", p=P, e=2))
             w1r.append(t1)
+
+        def load_x0(r, lo, n):
+            nc.sync.dma_start(out=xr0[r][:, lo * H : (lo + n) * H], in_=x_flat[r][:, lo * H : (lo + n) * H])
+
+        def load_w1(r, lo, n):
+            nc.sync.dma_start(out=w1r[r][:, lo : lo + n, :], in_=w1_view[r][:, lo : lo + n, :])
+
+        load_w1(0, 0, 2)
+        load_x0(0, 0, 2)
+        load_w1(0, 2, 2)
+        load_x0(0, 2, 2)
+        for r in range(1, R):
+            load_x0(r, 0, 4)
+            load_w1(r, 0, 4)
+        units = [(half, r) for half in range(2) for r in range(R)]
         w2r = []
-        for r in range(R):
-            t2 = big.tile([P, 4, H], BF16, name="w2r_%d" % r, tag="big")
-            nc.sync.dma_start(out=t2[:], in_=w_second[r].rearrange("(j p) n -> p j n", p=P))
+        for u in range(8):
+            t2 = w2p.tile([P, 4, 512], BF16, name="w2r_%d" % u, tag="w2r")
             w2r.append(t2)
+
+        def load_w2(u):
+            half, r = units[u]
+            nc.sync.dma_start(out=w2r[u][:], in_=w2_view[r][:, :, half * 512 : (half + 1) * 512])
+
+        for u in range(4):
+            load_w2(u)
 
         ident = const.tile([P, P], F32, name="ident")
         make_identity(nc, ident[:])
@@ -64,24 +91,37 @@ def tile_multilayerallreduce_pa_t_kernel(tc, x, w_first, w_second, out):
             else:
                 nc.scalar.copy(out=dst, in_=src)
 
-        def x_path(raw, a_lo, na, r, codes, scales, engines, tags):
+        def x_transpose(raw, a_lo, na, tags):
             words = raw[:].bitcast(F32)
-            grouped = xgp.tile([P, 2 * na * P * 4], BF16, name="xg", tag="xg", align_bytes=64)
-            gview = grouped[:].bitcast(F32).rearrange("p (g a m u) -> p g a m u", g=2, a=na, u=2)
+            banks = []
             for a in range(na):
                 bank = psum.tile([P, 4, P], F32, name="xt", tag=tags[a])
                 for s in range(4):
                     lo = (a_lo + a) * (H // 2) + s * P
                     nc.tensor.transpose(bank[:, s, :], words[:, lo : lo + P], ident[:])
-                copy_on(engines[a], gview[:, :, a, :, :], bank[:].rearrange("p (g u) m -> p g m u", g=2))
+                banks.append(bank)
+            return banks
+
+        def x_group(banks, engines):
+            na = len(banks)
+            grouped = xgp.tile([P, 2 * na * P * 4], BF16, name="xg", tag="xg", align_bytes=64)
+            gview = grouped[:].bitcast(F32).rearrange("p (g a m u) -> p g a m u", g=2, a=na, u=2)
+            for a in range(na):
+                copy_on(engines[a], gview[:, :, a, :, :], banks[a][:].rearrange("p (g u) m -> p g m u", g=2))
+            return grouped
+
+        def x_turn(raw, a_lo, na, engines, tags):
+            return x_group(x_transpose(raw, a_lo, na, tags), engines)
+
+        def x_quantise(grouped, r, codes, scales):
             nc.vector.quantize_mx(out=codes[:, r, :].bitcast(FP8X4), scales=scales[:, r, :], in_=grouped[:])
 
-        def w_regroup(src):
+        def w_regroup(src, vec_groups):
             grouped = wgp.tile([P, 4 * 512], BF16, name="wg", tag="wg", align_bytes=64)
             dv = grouped[:].rearrange("p (c i t) -> p c t i", i=4, t=4)
             sv = src.rearrange("p t (c i) -> p c t i", i=4)
-            nc.vector.tensor_copy(out=dv[:, 0:VEC_GROUPS, :, :], in_=sv[:, 0:VEC_GROUPS, :, :])
-            nc.scalar.copy(out=dv[:, VEC_GROUPS:P, :, :], in_=sv[:, VEC_GROUPS:P, :, :])
+            nc.vector.tensor_copy(out=dv[:, 0:vec_groups, :, :], in_=sv[:, 0:vec_groups, :, :])
+            nc.scalar.copy(out=dv[:, vec_groups:P, :, :], in_=sv[:, vec_groups:P, :, :])
             return grouped
 
         def w_quantise(grouped, codes, scales):
@@ -113,14 +153,39 @@ def tile_multilayerallreduce_pa_t_kernel(tc, x, w_first, w_second, out):
         xs0 = keep.tile([P, R, 1024], U8, name="xs0", align_bytes=64)
         acc1 = []
 
-        x_path(xr0[0], 0, 4, 0, xc0, xs0, "sssv", ["hi"] * 4)
+        def w1_rows(r, g):
+            return w1r[r][:].rearrange("p s (e f) -> p (s e) f", e=2)[:, 4 * g : 4 * g + 4, :]
+
+        def q1(r, g, grouped):
+            w_quantise(grouped, w1c[:, 2 * r + g, :], w1s[:, 2 * r + g, :])
+
+        wg0 = w_regroup(w1_rows(0, 0), VG0)
+        xb = x_transpose(xr0[0], 0, 4, ["hi"] * 4)
+        xgrp = xgp.tile([P, 2 * 4 * P * 4], BF16, name="xg", tag="xg", align_bytes=64)
+        gv = xgrp[:].bitcast(F32).rearrange("p (g a m u) -> p g a m u", g=2, a=4, u=2)
+
+        def ev0(a, e):
+            copy_on(e, gv[:, :, a, :, :], xb[a][:].rearrange("p (g u) m -> p g m u", g=2))
+
+        ev0(0, "s")
+        q1(0, 0, wg0)
+        ev0(1, "v")
+        wg1 = w_regroup(w1_rows(0, 1), VG0)
+        ev0(2, "s")
+        ev0(3, "v")
+        q1(0, 1, wg1)
+        xg = xgrp
         for r in range(R):
-            rows = w1r[r][:].rearrange("p s (e f) -> p (s e) f", e=2)
-            grouped = [w_regroup(rows[:, 4 * g : 4 * g + 4, :]) for g in range(2)]
-            for g in range(2):
-                w_quantise(grouped[g], w1c[:, 2 * r + g, :], w1s[:, 2 * r + g, :])
+            if r > 0:
+                wg0 = w_regroup(w1_rows(r, 0), VG1)
+                wg1 = w_regroup(w1_rows(r, 1), VG1)
+            x_quantise(xg, r, xc0, xs0)
+            if r > 0:
+                q1(r, 0, wg0)
             if r + 1 < R:
-                x_path(xr0[r + 1], 0, 4, r + 1, xc0, xs0, "sssv", ["hi"] * 4)
+                xg = x_turn(xr0[r + 1], 0, 4, X1_ENG, ["hi"] * 4)
+            if r > 0:
+                q1(r, 1, wg1)
             if r == 0:
                 for j in range(4):
                     acc_j = psum.tile([P, 512], F32, name="acc1_%d" % j, tag="lo")
@@ -133,108 +198,150 @@ def tile_multilayerallreduce_pa_t_kernel(tc, x, w_first, w_second, out):
         for r in range(R):
             t3 = xraw.tile([P, 4 * H], BF16, name="xr1_%d" % r, tag="xr")
             xr1.append(t3)
-        for c in range(2):
+
+        def load_x1(c):
             for r in range(R):
                 nc.sync.dma_start(
-                    out=xr1[r][:, 2 * c * H : (2 * c + 2) * H].rearrange("p (a h) -> p a h", a=2),
-                    in_=x_rows[r][:, 4 + 2 * c : 6 + 2 * c, :],
+                    out=xr1[r][:, 2 * c * H : (2 * c + 2) * H],
+                    in_=x_flat[r][:, (4 + 2 * c) * H : (6 + 2 * c) * H],
                 )
 
-        units = [(r, half) for r in range(R) for half in range(2)]
+        load_x1(0)
+        for u in range(4, 8):
+            load_w2(u)
+        load_x1(1)
 
-        def w2_regroup(u):
-            return w_regroup(w2r[units[u][0]][:, :, units[u][1] * 512 : (units[u][1] + 1) * 512])
-
-        rb = [None, None]
-        redq = [None, None]
-        acc2 = [[], []]
-        done = [0, 0]
-        nxt = w2_regroup(0)
-        for u in range(8):
-            cur = nxt
-            if u + 1 < 8:
-                nxt = w2_regroup(u + 1)
-            r, half = units[u]
-            w_quantise(cur, w2c[:, r, half * 512 : (half + 1) * 512], w2s[:, r, half * 512 : (half + 1) * 512])
-            for c in range(2):
-                if u == 1 + c:
-                    rb_c = red.tile([P, 4, 256], BF16, name="rb", tag="rb")
-                    for j in range(4):
-                        nc.scalar.copy(out=rb_c[:, j, :], in_=acc1[j][:, c * 256 : (c + 1) * 256])
-                    rb[c] = rb_c
-                if u == 2 + c:
-                    rg = red.tile([P, 4 * 256], BF16, name="rg", tag="rg", align_bytes=64)
-                    nc.vector.tensor_copy(
-                        out=rg[:].rearrange("p (c i t) -> p c t i", i=4, t=4),
-                        in_=rb[c][:].rearrange("p t (c i) -> p c t i", i=4),
-                    )
-                    rc = red.tile([P, 256], U32, name="rc", tag="rc", align_bytes=64)
-                    rs = red.tile([P, 256], U8, name="rs", tag="rs", align_bytes=64)
-                    nc.vector.quantize_mx(out=rc[:].bitcast(FP8X4), scales=rs[:], in_=rg[:])
-                    redq[c] = (rc, rs)
-                    for i in range(4):
-                        acc_i = psum.tile([P, 512], F32, name="acc2_%d_%d" % (c, i), tag=("hi", "lo")[c])
-                        acc2[c].append(acc_i)
-            ranks_ready = (u + 1) // 2
-            for c in range(2):
-                if redq[c] is not None:
-                    for rr in range(done[c], ranks_ready):
-                        for al in range(2):
-                            for hh in range(2):
-                                l2_pass(acc2[c][2 * al + hh][:], redq[c][0], redq[c][1], al * P, hh, rr)
-                    done[c] = ranks_ready
-
+        rb = keep.tile([P, 4, 512], BF16, name="rb")
+        rg = keep.tile([P, 4 * 512], BF16, name="rg", align_bytes=64)
+        rc = keep.tile([P, 512], U32, name="rc", align_bytes=64)
+        rs = keep.tile([P, 512], U8, name="rs", align_bytes=64)
+        xq = []
         for c in range(2):
-            ot = big.tile([P, 2, H], F32, name="ot", tag="big")
-            for al in range(2):
-                for hh in range(2):
-                    copy_on("sv"[hh], ot[:, al, hh * 512 : (hh + 1) * 512], acc2[c][2 * al + hh][:])
-            for r in range(R):
-                nc.sync.dma_start(out=out_rows[r][:, 2 * c : 2 * c + 2, :], in_=ot[:])
-
-        banks = [0]
-
-        def next_tag():
-            banks[0] += 1
-            return ("hi", "lo")[((banks[0] - 1) // 4) % 2]
-
-        def x_chunk(c):
             codes = keep.tile([P, R, 512], U32, name="xc_%d" % c, align_bytes=64)
             scales = keep.tile([P, R, 512], U8, name="xs_%d" % c, align_bytes=64)
-            for r in range(R):
-                x_path(xr1[r], 2 * (c - 2), 2, r, codes, scales, ("ss", "sv")[r % 2], [next_tag(), next_tag()])
-            return codes, scales
+            xq.append((codes, scales))
 
-        def l1_tile(q, al):
-            bank = psum.tile([P, 4, P], F32, name="acc1t", tag=next_tag())
+        def q2(u, grouped):
+            half, r = units[u]
+            w_quantise(grouped, w2c[:, r, half * 512 : (half + 1) * 512], w2s[:, r, half * 512 : (half + 1) * 512])
+
+        def store_half(oh, half, a_lo, n):
+            for r in range(R):
+                nc.sync.dma_start(
+                    out=out_rows[r][:, a_lo : a_lo + n, half * 512 : (half + 1) * 512],
+                    in_=oh[:, a_lo : a_lo + n, :],
+                )
+
+        def l1_tile(c, al, tag):
+            bank = psum.tile([P, 4, P], F32, name="acc1t", tag=tag)
             for j in range(4):
                 for r in range(R):
                     for g in range(2):
-                        l1_pass(bank[:, j, :], j, r, g, q[0], q[1], g * 256 + al * P, P)
-            rg = red.tile([P, 4 * P], BF16, name="rgt", tag="rgt", align_bytes=64)
-            nc.scalar.copy(out=rg[:].rearrange("p (m j) -> p m j", j=4), in_=bank[:].rearrange("p j m -> p m j"))
-            rc = red.tile([P, P], U32, name="rct", tag="rct", align_bytes=64)
-            rs = red.tile([P, P], U8, name="rst", tag="rst", align_bytes=64)
-            nc.vector.quantize_mx(out=rc[:].bitcast(FP8X4), scales=rs[:], in_=rg[:])
-            return rc, rs
+                        l1_pass(bank[:, j, :], j, r, g, xq[c][0], xq[c][1], g * 256 + al * P, P)
+            return bank
 
-        def l2_tile(rq, ot, al):
+        def red_tile(bank):
+            rgt = red.tile([P, 4 * P], BF16, name="rgt", tag="rgt", align_bytes=64)
+            nc.scalar.copy(out=rgt[:].rearrange("p (m j) -> p m j", j=4), in_=bank[:].rearrange("p j m -> p m j"))
+            rct = red.tile([P, P], U32, name="rct", tag="rct", align_bytes=64)
+            rst = red.tile([P, P], U8, name="rst", tag="rst", align_bytes=64)
+            nc.vector.quantize_mx(out=rct[:].bitcast(FP8X4), scales=rst[:], in_=rgt[:])
+            return rct, rst
+
+        def l2_tile(rq, ot, al, tags, engines):
             for hh in range(2):
-                acc = psum.tile([P, 512], F32, name="acc2t", tag=next_tag())
+                acc = psum.tile([P, 512], F32, name="acc2t", tag=tags[hh])
                 for r in range(R):
                     l2_pass(acc[:], rq[0], rq[1], 0, hh, r)
-                copy_on("sv"[hh], ot[:, al, hh * 512 : (hh + 1) * 512], acc[:])
+                copy_on(engines[hh], ot[:, al, hh * 512 : (hh + 1) * 512], acc[:])
 
-        q2 = x_chunk(2)
-        q3 = x_chunk(3)
-        for c, q in ((2, q2), (3, q3)):
-            rq = [l1_tile(q, al) for al in range(2)]
-            ot = big.tile([P, 2, H], F32, name="ot", tag="big")
-            for al in range(2):
-                l2_tile(rq[al], ot, al)
-                if c == 3:
-                    for r in range(R):
-                        nc.sync.dma_start(out=out_rows[r][:, 2 * c + al, :], in_=ot[:, al, :])
-            if c == 2:
-                for r in range(R):
-                    nc.sync.dma_start(out=out_rows[r][:, 2 * c : 2 * c + 2, :], in_=ot[:])
+        g0 = w_regroup(w2r[0][:], VG2)
+        g1 = w_regroup(w2r[1][:], VG2)
+        q2(0, g0)
+        xb0 = x_transpose(xr1[0], 0, 2, ["hi", "hi"])
+        xb1 = x_transpose(xr1[1], 0, 2, ["hi", "hi"])
+        for j in range(4):
+            copy_on(RB_ENG[j], rb[:, j, :], acc1[j][:])
+        g2 = w_regroup(w2r[2][:], VG2)
+        q2(1, g1)
+        nc.vector.tensor_copy(
+            out=rg[:].rearrange("p (c i t) -> p c t i", i=4, t=4),
+            in_=rb[:].rearrange("p t (c i) -> p c t i", i=4),
+        )
+        g3 = w_regroup(w2r[3][:], VG2)
+        q2(2, g2)
+        nc.vector.quantize_mx(out=rc[:].bitcast(FP8X4), scales=rs[:], in_=rg[:])
+        q2(3, g3)
+        oh0 = big.tile([P, 4, 512], F32, name="oh0", tag="big")
+        acc2 = []
+        for a in range(4):
+            acc_a = psum.tile([P, 512], F32, name="acc2_0_%d" % a, tag="lo")
+            acc2.append(acc_a)
+            for rr in range(R):
+                l2_pass(acc_a[:], rc, rs, a * P, 0, rr)
+        g4 = w_regroup(w2r[4][:], VG3)
+        xg0 = x_group(xb0, "ss")
+        g5 = w_regroup(w2r[5][:], VG3)
+        q2(4, g4)
+        xg1 = x_group(xb1, "ss")
+        xb2 = x_transpose(xr1[2], 0, 2, ["hi", "hi"])
+        xb3 = x_transpose(xr1[3], 0, 2, ["hi", "hi"])
+        for a in range(4):
+            copy_on(H0_ENG[a], oh0[:, a, :], acc2[a][:])
+            if a % 2 == 1:
+                store_half(oh0, 0, a - 1, 2)
+        g6 = w_regroup(w2r[6][:], VG3)
+        q2(5, g5)
+        x_quantise(xg0, 0, xq[0][0], xq[0][1])
+        g7 = w_regroup(w2r[7][:], VG3)
+        q2(6, g6)
+        x_quantise(xg1, 1, xq[0][0], xq[0][1])
+        q2(7, g7)
+        oh1 = big.tile([P, 4, 512], F32, name="oh1", tag="big")
+        acc2 = []
+        for a in range(4):
+            acc_a = psum.tile([P, 512], F32, name="acc2_1_%d" % a, tag="lo")
+            acc2.append(acc_a)
+        for rr in range(R):
+            for a in range(4):
+                l2_pass(acc2[a][:], rc, rs, a * P, 1, rr)
+        xg2 = x_group(xb2, "ss")
+        xg3 = x_group(xb3, "ss")
+        x_quantise(xg2, 2, xq[0][0], xq[0][1])
+        for a in range(4):
+            copy_on(H1_ENG[a], oh1[:, a, :], acc2[a][:])
+            if a % 2 == 1:
+                store_half(oh1, 1, a - 1, 2)
+        x_quantise(xg3, 3, xq[0][0], xq[0][1])
+        xb0 = x_transpose(xr1[0], 2, 2, ["hi", "hi"])
+        xb1 = x_transpose(xr1[1], 2, 2, ["hi", "hi"])
+        bank0 = l1_tile(0, 0, "lo")
+        bank1 = l1_tile(0, 1, "lo")
+        xg0 = x_group(xb0, "sv")
+        xg1 = x_group(xb1, "sv")
+        rq0 = red_tile(bank0)
+        x_quantise(xg0, 0, xq[1][0], xq[1][1])
+        rq1 = red_tile(bank1)
+        x_quantise(xg1, 1, xq[1][0], xq[1][1])
+        xb2 = x_transpose(xr1[2], 2, 2, ["hi", "hi"])
+        xb3 = x_transpose(xr1[3], 2, 2, ["hi", "hi"])
+        ot = big.tile([P, 2, H], F32, name="ot", tag="big")
+        xg2 = x_group(xb2, "sv")
+        xg3 = x_group(xb3, "sv")
+        l2_tile(rq0, ot, 0, ["lo", "lo"], "sv")
+        for r in range(R):
+            nc.sync.dma_start(out=out_rows[r][:, 4, :], in_=ot[:, 0, :])
+        x_quantise(xg2, 2, xq[1][0], xq[1][1])
+        x_quantise(xg3, 3, xq[1][0], xq[1][1])
+        l2_tile(rq1, ot, 1, ["hi", "hi"], "sv")
+        for r in range(R):
+            nc.sync.dma_start(out=out_rows[r][:, 5, :], in_=ot[:, 1, :])
+        bank0 = l1_tile(1, 0, "hi")
+        rq0 = red_tile(bank0)
+        bank1 = l1_tile(1, 1, "hi")
+        rq1 = red_tile(bank1)
+        ot = big.tile([P, 2, H], F32, name="ot", tag="big")
+        for al, rq in ((0, rq0), (1, rq1)):
+            l2_tile(rq, ot, al, ["lo", "lo"], "sv")
+            for r in range(R):
+                nc.sync.dma_start(out=out_rows[r][:, 6 + al, :], in_=ot[:, al, :])

@@ -30,8 +30,7 @@ def tile_multilayerallreduce_pa_t_kernel(tc, x, w_first, w_second, out):
         ctx.enter_context(tc.manual_schedule())
         const = ctx.enter_context(tc.tile_pool(name="const", bufs=1))
         xraw = ctx.enter_context(tc.tile_pool(name="xraw", bufs=4))
-        big = ctx.enter_context(tc.tile_pool(name="big", bufs=4))
-        w2p = ctx.enter_context(tc.tile_pool(name="w2p", bufs=8))
+        big = ctx.enter_context(tc.tile_pool(name="big", bufs=8))
         xgp = ctx.enter_context(tc.tile_pool(name="xgp", bufs=2))
         wgp = ctx.enter_context(tc.tile_pool(name="wgp", bufs=3))
         keep = ctx.enter_context(tc.tile_pool(name="keep", bufs=1))
@@ -41,7 +40,7 @@ def tile_multilayerallreduce_pa_t_kernel(tc, x, w_first, w_second, out):
         x_flat = [x[r].rearrange("(m a) h -> m (a h)", a=A) for r in range(R)]
         out_rows = [out[r].rearrange("(m a) n -> m a n", a=A) for r in range(R)]
         w1_view = [w_first[r].rearrange("(s p e) f -> p s (e f)", p=P, e=2) for r in range(R)]
-        w2_view = [w_second[r].rearrange("(j p) n -> p j n", p=P) for r in range(R)]
+        w2_view = [w_second[r].rearrange("(p j) n -> p j n", j=4) for r in range(R)]
 
         xr0 = []
         w1r = []
@@ -65,17 +64,12 @@ def tile_multilayerallreduce_pa_t_kernel(tc, x, w_first, w_second, out):
             load_x0(r, 0, 4)
             load_w1(r, 0, 4)
         units = [(half, r) for half in range(2) for r in range(R)]
-        w2r = []
-        for u in range(8):
-            t2 = w2p.tile([P, 4, 512], BF16, name="w2r_%d" % u, tag="w2r")
-            w2r.append(t2)
-
-        def load_w2(u):
-            half, r = units[u]
-            nc.sync.dma_start(out=w2r[u][:], in_=w2_view[r][:, :, half * 512 : (half + 1) * 512])
-
-        for u in range(4):
-            load_w2(u)
+        w2full = []
+        for r in range(R):
+            t2 = big.tile([P, 4, H], BF16, name="w2r_%d" % r, tag="big")
+            nc.sync.dma_start(out=t2[:], in_=w2_view[r])
+            w2full.append(t2)
+        w2r = [w2full[r][:, :, half * 512 : (half + 1) * 512] for half, r in units]
 
         ident = const.tile([P, P], F32, name="ident")
         make_identity(nc, ident[:])
@@ -124,6 +118,14 @@ def tile_multilayerallreduce_pa_t_kernel(tc, x, w_first, w_second, out):
             nc.scalar.copy(out=dv[:, vec_groups:P, :, :], in_=sv[:, vec_groups:P, :, :])
             return grouped
 
+        def w1_regroup(src, vec_cols):
+            grouped = wgp.tile([P, 4 * 512], BF16, name="wg", tag="wg", align_bytes=64)
+            dv = grouped[:].rearrange("p (j m t) -> p j m t", j=4, t=4)
+            sv = src.rearrange("p t (m j) -> p j m t", j=4)
+            nc.vector.tensor_copy(out=dv[:, :, 0:vec_cols, :], in_=sv[:, :, 0:vec_cols, :])
+            nc.scalar.copy(out=dv[:, :, vec_cols:P, :], in_=sv[:, :, vec_cols:P, :])
+            return grouped
+
         def w_quantise(grouped, codes, scales):
             nc.vector.quantize_mx(out=codes.bitcast(FP8X4), scales=scales, in_=grouped[:])
 
@@ -159,7 +161,7 @@ def tile_multilayerallreduce_pa_t_kernel(tc, x, w_first, w_second, out):
         def q1(r, g, grouped):
             w_quantise(grouped, w1c[:, 2 * r + g, :], w1s[:, 2 * r + g, :])
 
-        wg0 = w_regroup(w1_rows(0, 0), VG0)
+        wg0 = w1_regroup(w1_rows(0, 0), VG0)
         xb = x_transpose(xr0[0], 0, 4, ["hi"] * 4)
         xgrp = xgp.tile([P, 2 * 4 * P * 4], BF16, name="xg", tag="xg", align_bytes=64)
         gv = xgrp[:].bitcast(F32).rearrange("p (g a m u) -> p g a m u", g=2, a=4, u=2)
@@ -170,15 +172,15 @@ def tile_multilayerallreduce_pa_t_kernel(tc, x, w_first, w_second, out):
         ev0(0, "s")
         q1(0, 0, wg0)
         ev0(1, "v")
-        wg1 = w_regroup(w1_rows(0, 1), VG0)
+        wg1 = w1_regroup(w1_rows(0, 1), VG0)
         ev0(2, "s")
         ev0(3, "v")
         q1(0, 1, wg1)
         xg = xgrp
         for r in range(R):
             if r > 0:
-                wg0 = w_regroup(w1_rows(r, 0), VG1)
-                wg1 = w_regroup(w1_rows(r, 1), VG1)
+                wg0 = w1_regroup(w1_rows(r, 0), VG1)
+                wg1 = w1_regroup(w1_rows(r, 1), VG1)
             x_quantise(xg, r, xc0, xs0)
             if r > 0:
                 q1(r, 0, wg0)
@@ -207,8 +209,6 @@ def tile_multilayerallreduce_pa_t_kernel(tc, x, w_first, w_second, out):
                 )
 
         load_x1(0)
-        for u in range(4, 8):
-            load_w2(u)
         load_x1(1)
 
         rb = keep.tile([P, 4, 512], BF16, name="rb")
@@ -255,20 +255,20 @@ def tile_multilayerallreduce_pa_t_kernel(tc, x, w_first, w_second, out):
                     l2_pass(acc[:], rq[0], rq[1], 0, hh, r)
                 copy_on(engines[hh], ot[:, al, hh * 512 : (hh + 1) * 512], acc[:])
 
-        g0 = w_regroup(w2r[0][:], VG2)
-        g1 = w_regroup(w2r[1][:], VG2)
+        g0 = w_regroup(w2r[0], VG2)
+        g1 = w_regroup(w2r[1], VG2)
         q2(0, g0)
         xb0 = x_transpose(xr1[0], 0, 2, ["hi", "hi"])
         xb1 = x_transpose(xr1[1], 0, 2, ["hi", "hi"])
         for j in range(4):
             copy_on(RB_ENG[j], rb[:, j, :], acc1[j][:])
-        g2 = w_regroup(w2r[2][:], VG2)
+        g2 = w_regroup(w2r[2], VG2)
         q2(1, g1)
         nc.vector.tensor_copy(
             out=rg[:].rearrange("p (c i t) -> p c t i", i=4, t=4),
             in_=rb[:].rearrange("p t (c i) -> p c t i", i=4),
         )
-        g3 = w_regroup(w2r[3][:], VG2)
+        g3 = w_regroup(w2r[3], VG2)
         q2(2, g2)
         nc.vector.quantize_mx(out=rc[:].bitcast(FP8X4), scales=rs[:], in_=rg[:])
         q2(3, g3)
@@ -279,9 +279,9 @@ def tile_multilayerallreduce_pa_t_kernel(tc, x, w_first, w_second, out):
             acc2.append(acc_a)
             for rr in range(R):
                 l2_pass(acc_a[:], rc, rs, a * P, 0, rr)
-        g4 = w_regroup(w2r[4][:], VG3)
+        g4 = w_regroup(w2r[4], VG3)
         xg0 = x_group(xb0, "ss")
-        g5 = w_regroup(w2r[5][:], VG3)
+        g5 = w_regroup(w2r[5], VG3)
         q2(4, g4)
         xg1 = x_group(xb1, "ss")
         xb2 = x_transpose(xr1[2], 0, 2, ["hi", "hi"])
@@ -290,10 +290,10 @@ def tile_multilayerallreduce_pa_t_kernel(tc, x, w_first, w_second, out):
             copy_on(H0_ENG[a], oh0[:, a, :], acc2[a][:])
             if a % 2 == 1:
                 store_half(oh0, 0, a - 1, 2)
-        g6 = w_regroup(w2r[6][:], VG3)
+        g6 = w_regroup(w2r[6], VG3)
         q2(5, g5)
         x_quantise(xg0, 0, xq[0][0], xq[0][1])
-        g7 = w_regroup(w2r[7][:], VG3)
+        g7 = w_regroup(w2r[7], VG3)
         q2(6, g6)
         x_quantise(xg1, 1, xq[0][0], xq[0][1])
         q2(7, g7)

@@ -14,6 +14,8 @@ R, T, H, F = 4, 1024, 1024, 512
 A = T // P
 FLOPS = 2 * R * T * H * F * 2
 
+B03 = ["b0", "b1", "b2", "b3"]
+B47 = ["b4", "b5", "b6", "b7"]
 VG0 = 64
 VG1 = 64
 X1_ENG = "vsss"
@@ -35,7 +37,7 @@ def tile_multilayerallreduce_pa_t_kernel(tc, x, w_first, w_second, out):
         wgp = ctx.enter_context(tc.tile_pool(name="wgp", bufs=3))
         keep = ctx.enter_context(tc.tile_pool(name="keep", bufs=1))
         red = ctx.enter_context(tc.tile_pool(name="red", bufs=2))
-        psum = ctx.enter_context(tc.psum_pool(name="psum", bufs=4))
+        psum = ctx.enter_context(tc.psum_pool(name="psum", bufs=1))
 
         x_flat = [x[r].rearrange("(m a) h -> m (a h)", a=A) for r in range(R)]
         out_rows = [out[r].rearrange("(m a) n -> m a n", a=A) for r in range(R)]
@@ -140,6 +142,17 @@ def tile_multilayerallreduce_pa_t_kernel(tc, x, w_first, w_second, out):
                 stop=(r == R - 1 and g == 1),
             )
 
+        def l1_open_pass(acc, j, r, g, lo):
+            nc.tensor.matmul_mx(
+                out=acc,
+                lhsT=w1c[:, 2 * r + g, j * P : (j + 1) * P].bitcast(FP8X4),
+                lhsT_scale=w1s[:, 2 * r + g, j * P : (j + 1) * P],
+                rhs=xc0[:, r, lo : lo + P].bitcast(FP8X4),
+                rhs_scale=xs0[:, r, lo : lo + P],
+                start=(r == 0 and g == 0 and j == 0),
+                stop=(r == R - 1 and g == 1 and j == 3),
+            )
+
         def l2_pass(acc, rc, rs, lo, half, r):
             nc.tensor.matmul_mx(
                 out=acc,
@@ -162,7 +175,7 @@ def tile_multilayerallreduce_pa_t_kernel(tc, x, w_first, w_second, out):
             w_quantise(grouped, w1c[:, 2 * r + g, :], w1s[:, 2 * r + g, :])
 
         wg0 = w1_regroup(w1_rows(0, 0), VG0)
-        xb = x_transpose(xr0[0], 0, 4, ["hi"] * 4)
+        xb = x_transpose(xr0[0], 0, 4, B03)
         xgrp = xgp.tile([P, 2 * 4 * P * 4], BF16, name="xg", tag="xg", align_bytes=64)
         gv = xgrp[:].bitcast(F32).rearrange("p (g a m u) -> p g a m u", g=2, a=4, u=2)
 
@@ -185,16 +198,17 @@ def tile_multilayerallreduce_pa_t_kernel(tc, x, w_first, w_second, out):
             if r > 0:
                 q1(r, 0, wg0)
             if r + 1 < R:
-                xg = x_turn(xr0[r + 1], 0, 4, X1_ENG, ["hi"] * 4)
+                xg = x_turn(xr0[r + 1], 0, 4, X1_ENG, B03)
             if r > 0:
                 q1(r, 1, wg1)
             if r == 0:
-                for j in range(4):
-                    acc_j = psum.tile([P, 512], F32, name="acc1_%d" % j, tag="lo")
-                    acc1.append(acc_j)
+                for a in range(4):
+                    acc_a = psum.tile([P, 4, P], F32, name="acc1_%d" % a, tag=B47[a])
+                    acc1.append(acc_a)
             for g in range(2):
                 for j in range(4):
-                    l1_pass(acc1[j][:], j, r, g, xc0, xs0, g * 512, 512)
+                    for a in range(4):
+                        l1_open_pass(acc1[a][:, j, :], j, r, g, g * 512 + a * P)
 
         xr1 = []
         for r in range(R):
@@ -211,10 +225,6 @@ def tile_multilayerallreduce_pa_t_kernel(tc, x, w_first, w_second, out):
         load_x1(0)
         load_x1(1)
 
-        rb = keep.tile([P, 4, 512], BF16, name="rb")
-        rg = keep.tile([P, 4 * 512], BF16, name="rg", align_bytes=64)
-        rc = keep.tile([P, 512], U32, name="rc", align_bytes=64)
-        rs = keep.tile([P, 512], U8, name="rs", align_bytes=64)
         xq = []
         for c in range(2):
             codes = keep.tile([P, R, 512], U32, name="xc_%d" % c, align_bytes=64)
@@ -255,93 +265,118 @@ def tile_multilayerallreduce_pa_t_kernel(tc, x, w_first, w_second, out):
                     l2_pass(acc[:], rq[0], rq[1], 0, hh, r)
                 copy_on(engines[hh], ot[:, al, hh * 512 : (hh + 1) * 512], acc[:])
 
+        def xq_(c, r, grouped):
+            x_quantise(grouped, r, xq[c][0], xq[c][1])
+
+        def red0_copy(a):
+            rgt = keep.tile([P, 4 * P], BF16, name="rg0_%d" % a, align_bytes=64)
+            nc.scalar.copy(out=rgt[:].rearrange("p (m j) -> p m j", j=4), in_=acc1[a][:].rearrange("p j m -> p m j"))
+            return rgt
+
+        def red0_quantise(a, rgt):
+            rct = keep.tile([P, P], U32, name="rc0_%d" % a, align_bytes=64)
+            rst = keep.tile([P, P], U8, name="rs0_%d" % a, align_bytes=64)
+            nc.vector.quantize_mx(out=rct[:].bitcast(FP8X4), scales=rst[:], in_=rgt[:])
+            return rct, rst
+
+        def open_banks(tags):
+            accs = []
+            for i in range(len(tags)):
+                acc_i = psum.tile([P, 512], F32, name="acc2", tag=tags[i])
+                accs.append(acc_i)
+            return accs
+
+        def l2_tiles(accs, tiles, half, rr):
+            for a in tiles:
+                l2_pass(accs[a][:], rq0s[a][0], rq0s[a][1], 0, half, rr)
+
+        def out_half(accs, oh, half, engines):
+            for a in range(4):
+                copy_on(engines[a], oh[:, a, :], accs[a][:])
+                if a % 2 == 1:
+                    store_half(oh, half, a - 1, 2)
+
         g0 = w_regroup(w2r[0], VG2)
         g1 = w_regroup(w2r[1], VG2)
         q2(0, g0)
-        xb0 = x_transpose(xr1[0], 0, 2, ["hi", "hi"])
-        xb1 = x_transpose(xr1[1], 0, 2, ["hi", "hi"])
-        for j in range(4):
-            copy_on(RB_ENG[j], rb[:, j, :], acc1[j][:])
-        g2 = w_regroup(w2r[2], VG2)
+        rgs = [red0_copy(a) for a in range(4)]
+        rq0s = []
         q2(1, g1)
-        nc.vector.tensor_copy(
-            out=rg[:].rearrange("p (c i t) -> p c t i", i=4, t=4),
-            in_=rb[:].rearrange("p t (c i) -> p c t i", i=4),
-        )
+        rq0s.append(red0_quantise(0, rgs[0]))
+        rq0s.append(red0_quantise(1, rgs[1]))
+        g2 = w_regroup(w2r[2], VG2)
+        rq0s.append(red0_quantise(2, rgs[2]))
+        rq0s.append(red0_quantise(3, rgs[3]))
         g3 = w_regroup(w2r[3], VG2)
         q2(2, g2)
-        nc.vector.quantize_mx(out=rc[:].bitcast(FP8X4), scales=rs[:], in_=rg[:])
         q2(3, g3)
-        oh0 = big.tile([P, 4, 512], F32, name="oh0", tag="big")
-        acc2 = []
-        for a in range(4):
-            acc_a = psum.tile([P, 512], F32, name="acc2_0_%d" % a, tag="lo")
-            acc2.append(acc_a)
-            for rr in range(R):
-                l2_pass(acc_a[:], rc, rs, a * P, 0, rr)
+        h0 = open_banks(B03)
+        l2_tiles(h0, (0, 1), 0, 0)
+        l2_tiles(h0, (0, 1), 0, 1)
+        l2_tiles(h0, (2, 3), 0, 0)
+        l2_tiles(h0, (2, 3), 0, 1)
+        l2_tiles(h0, (0, 1, 2, 3), 0, 2)
+        l2_tiles(h0, (0, 1, 2, 3), 0, 3)
+        xb0 = x_transpose(xr1[0], 0, 2, ["b4", "b5"])
+        xb1 = x_transpose(xr1[1], 0, 2, ["b6", "b7"])
         g4 = w_regroup(w2r[4], VG3)
-        xg0 = x_group(xb0, "ss")
         g5 = w_regroup(w2r[5], VG3)
         q2(4, g4)
-        xg1 = x_group(xb1, "ss")
-        xb2 = x_transpose(xr1[2], 0, 2, ["hi", "hi"])
-        xb3 = x_transpose(xr1[3], 0, 2, ["hi", "hi"])
-        for a in range(4):
-            copy_on(H0_ENG[a], oh0[:, a, :], acc2[a][:])
-            if a % 2 == 1:
-                store_half(oh0, 0, a - 1, 2)
+        oh0 = big.tile([P, 4, 512], F32, name="oh0", tag="big")
+        out_half(h0, oh0, 0, H0_ENG)
         g6 = w_regroup(w2r[6], VG3)
         q2(5, g5)
-        x_quantise(xg0, 0, xq[0][0], xq[0][1])
+        xg0 = x_group(xb0, "ss")
         g7 = w_regroup(w2r[7], VG3)
         q2(6, g6)
-        x_quantise(xg1, 1, xq[0][0], xq[0][1])
+        xg1 = x_group(xb1, "ss")
+        xq_(0, 0, xg0)
         q2(7, g7)
-        oh1 = big.tile([P, 4, 512], F32, name="oh1", tag="big")
-        acc2 = []
-        for a in range(4):
-            acc_a = psum.tile([P, 512], F32, name="acc2_1_%d" % a, tag="lo")
-            acc2.append(acc_a)
-        for rr in range(R):
-            for a in range(4):
-                l2_pass(acc2[a][:], rc, rs, a * P, 1, rr)
+        xq_(0, 1, xg1)
+        h1 = open_banks(B03)
+        for rr in range(2):
+            l2_tiles(h1, (0, 1, 2, 3), 1, rr)
+        xb2 = x_transpose(xr1[2], 0, 2, ["b4", "b5"])
+        xb3 = x_transpose(xr1[3], 0, 2, ["b6", "b7"])
+        for rr in range(2, 4):
+            l2_tiles(h1, (0, 1, 2, 3), 1, rr)
         xg2 = x_group(xb2, "ss")
-        xg3 = x_group(xb3, "ss")
-        x_quantise(xg2, 2, xq[0][0], xq[0][1])
-        for a in range(4):
-            copy_on(H1_ENG[a], oh1[:, a, :], acc2[a][:])
-            if a % 2 == 1:
-                store_half(oh1, 1, a - 1, 2)
-        x_quantise(xg3, 3, xq[0][0], xq[0][1])
-        xb0 = x_transpose(xr1[0], 2, 2, ["hi", "hi"])
-        xb1 = x_transpose(xr1[1], 2, 2, ["hi", "hi"])
-        bank0 = l1_tile(0, 0, "lo")
-        bank1 = l1_tile(0, 1, "lo")
-        xg0 = x_group(xb0, "sv")
-        xg1 = x_group(xb1, "sv")
-        rq0 = red_tile(bank0)
-        x_quantise(xg0, 0, xq[1][0], xq[1][1])
-        rq1 = red_tile(bank1)
-        x_quantise(xg1, 1, xq[1][0], xq[1][1])
-        xb2 = x_transpose(xr1[2], 2, 2, ["hi", "hi"])
-        xb3 = x_transpose(xr1[3], 2, 2, ["hi", "hi"])
-        ot = big.tile([P, 2, H], F32, name="ot", tag="big")
-        xg2 = x_group(xb2, "sv")
         xg3 = x_group(xb3, "sv")
-        l2_tile(rq0, ot, 0, ["lo", "lo"], "sv")
+        xq_(0, 2, xg2)
+        xq_(0, 3, xg3)
+        oh1 = big.tile([P, 4, 512], F32, name="oh1", tag="big")
+        out_half(h1, oh1, 1, H1_ENG)
+        xb0 = x_transpose(xr1[0], 2, 2, ["b6", "b7"])
+        bank0 = l1_tile(0, 0, "b4")
+        bank1 = l1_tile(0, 1, "b5")
+        xb1 = x_transpose(xr1[1], 2, 2, ["b0", "b1"])
+        xb2 = x_transpose(xr1[2], 2, 2, ["b2", "b3"])
+        xg0 = x_group(xb0, "sv")
+        rq0 = red_tile(bank0)
+        xq_(1, 0, xg0)
+        xg1 = x_group(xb1, "sv")
+        rq1 = red_tile(bank1)
+        xq_(1, 1, xg1)
+        xg2 = x_group(xb2, "sv")
+        xb3 = x_transpose(xr1[3], 2, 2, ["b6", "b7"])
+        xq_(1, 2, xg2)
+        xg3 = x_group(xb3, "sv")
+        ot = big.tile([P, 2, H], F32, name="ot", tag="big")
+        l2_tile(rq0, ot, 0, ["b4", "b5"], "sv")
         for r in range(R):
             nc.sync.dma_start(out=out_rows[r][:, 4, :], in_=ot[:, 0, :])
-        x_quantise(xg2, 2, xq[1][0], xq[1][1])
-        x_quantise(xg3, 3, xq[1][0], xq[1][1])
-        l2_tile(rq1, ot, 1, ["hi", "hi"], "sv")
+        xq_(1, 3, xg3)
+        l2_tile(rq1, ot, 1, ["b0", "b1"], "sv")
         for r in range(R):
             nc.sync.dma_start(out=out_rows[r][:, 5, :], in_=ot[:, 1, :])
-        bank0 = l1_tile(1, 0, "hi")
+        bank0 = l1_tile(1, 0, "b2")
         rq0 = red_tile(bank0)
-        bank1 = l1_tile(1, 1, "hi")
+        bank1 = l1_tile(1, 1, "b3")
         rq1 = red_tile(bank1)
         ot = big.tile([P, 2, H], F32, name="ot", tag="big")
-        for al, rq in ((0, rq0), (1, rq1)):
-            l2_tile(rq, ot, al, ["lo", "lo"], "sv")
-            for r in range(R):
-                nc.sync.dma_start(out=out_rows[r][:, 6 + al, :], in_=ot[:, al, :])
+        l2_tile(rq0, ot, 0, ["b4", "b5"], "sv")
+        for r in range(R):
+            nc.sync.dma_start(out=out_rows[r][:, 6, :], in_=ot[:, 0, :])
+        l2_tile(rq1, ot, 1, ["b6", "b7"], "sv")
+        for r in range(R):
+            nc.sync.dma_start(out=out_rows[r][:, 7, :], in_=ot[:, 1, :])

@@ -40,7 +40,7 @@ def tile_multilayerallreduce_pa_t_kernel(tc, x, w_first, w_second, out):
         psum = ctx.enter_context(tc.psum_pool(name="psum", bufs=1))
 
         x_flat = [x[r].rearrange("(m a) h -> m (a h)", a=A) for r in range(R)]
-        out_rows = [out[r].rearrange("(m a) n -> m a n", a=A) for r in range(R)]
+        out_all = out.rearrange("r (m a) n -> m r a n", a=A)
         w1_view = [w_first[r].rearrange("(s p e) f -> p s (e f)", p=P, e=2) for r in range(R)]
         w2_view = [w_second[r].rearrange("(p j) n -> p j n", j=4) for r in range(R)]
 
@@ -236,10 +236,10 @@ def tile_multilayerallreduce_pa_t_kernel(tc, x, w_first, w_second, out):
             w_quantise(grouped, w2c[:, r, half * 512 : (half + 1) * 512], w2s[:, r, half * 512 : (half + 1) * 512])
 
         def store_half(oh, half, a_lo, n):
-            for r in range(R):
+            for a in range(a_lo, a_lo + n):
                 nc.sync.dma_start(
-                    out=out_rows[r][:, a_lo : a_lo + n, half * 512 : (half + 1) * 512],
-                    in_=oh[:, a_lo : a_lo + n, :],
+                    out=out_all[:, :, a, half * 512 : (half + 1) * 512],
+                    in_=oh[:, a, :].unsqueeze(1).to_broadcast([P, R, 512]),
                 )
 
         def l1_tile(c, al, tag):
@@ -363,20 +363,16 @@ def tile_multilayerallreduce_pa_t_kernel(tc, x, w_first, w_second, out):
         xg3 = x_group(xb3, "sv")
         ot = big.tile([P, 2, H], F32, name="ot", tag="big")
         l2_tile(rq0, ot, 0, ["b4", "b5"], "sv")
-        for r in range(R):
-            nc.sync.dma_start(out=out_rows[r][:, 4, :], in_=ot[:, 0, :])
+        nc.sync.dma_start(out=out_all[:, :, 4, :], in_=ot[:, 0, :].unsqueeze(1).to_broadcast([P, R, H]))
         xq_(1, 3, xg3)
         l2_tile(rq1, ot, 1, ["b0", "b1"], "sv")
-        for r in range(R):
-            nc.sync.dma_start(out=out_rows[r][:, 5, :], in_=ot[:, 1, :])
+        nc.sync.dma_start(out=out_all[:, :, 5, :], in_=ot[:, 1, :].unsqueeze(1).to_broadcast([P, R, H]))
         bank0 = l1_tile(1, 0, "b2")
         rq0 = red_tile(bank0)
         bank1 = l1_tile(1, 1, "b3")
         rq1 = red_tile(bank1)
         ot = big.tile([P, 2, H], F32, name="ot", tag="big")
         l2_tile(rq0, ot, 0, ["b4", "b5"], "sv")
-        for r in range(R):
-            nc.sync.dma_start(out=out_rows[r][:, 6, :], in_=ot[:, 0, :])
+        nc.sync.dma_start(out=out_all[:, :, 6, :], in_=ot[:, 0, :].unsqueeze(1).to_broadcast([P, R, H]))
         l2_tile(rq1, ot, 1, ["b6", "b7"], "sv")
-        for r in range(R):
-            nc.sync.dma_start(out=out_rows[r][:, 7, :], in_=ot[:, 1, :])
+        nc.sync.dma_start(out=out_all[:, :, 7, :], in_=ot[:, 1, :].unsqueeze(1).to_broadcast([P, R, H]))

@@ -19,8 +19,8 @@ B47 = ["b4", "b5", "b6", "b7"]
 VG0 = 64
 VG1 = 64
 X1_ENG = "vsss"
-VG2 = 64
-VG3 = 64
+VG2 = 80
+VG3 = 80
 RB_ENG = "ssvv"
 H0_ENG = "svsv"
 H1_ENG = "svsv"
@@ -41,6 +41,7 @@ def tile_multilayerallreduce_pa_t_kernel(tc, x, w_first, w_second, out):
 
         x_flat = [x[r].rearrange("(m a) h -> m (a h)", a=A) for r in range(R)]
         out_all = out.rearrange("r (m a) n -> m r a n", a=A)
+        out_flat = out.rearrange("r (m a) n -> m r (a n)", a=A)
         w1_view = [w_first[r].rearrange("(s p e) f -> p s (e f)", p=P, e=2) for r in range(R)]
         w2_view = [w_second[r].rearrange("(p j) n -> p j n", j=4) for r in range(R)]
 
@@ -222,8 +223,8 @@ def tile_multilayerallreduce_pa_t_kernel(tc, x, w_first, w_second, out):
                     in_=x_flat[r][:, (4 + 2 * c) * H : (6 + 2 * c) * H],
                 )
 
-        load_x1(0)
-        load_x1(1)
+        for r in range(R):
+            nc.sync.dma_start(out=xr1[r][:], in_=x_flat[r][:, 4 * H : 8 * H])
 
         xq = []
         for c in range(2):
@@ -235,13 +236,6 @@ def tile_multilayerallreduce_pa_t_kernel(tc, x, w_first, w_second, out):
             half, r = units[u]
             w_quantise(grouped, w2c[:, r, half * 512 : (half + 1) * 512], w2s[:, r, half * 512 : (half + 1) * 512])
 
-        def store_half(oh, half, a_lo, n):
-            for a in range(a_lo, a_lo + n):
-                nc.sync.dma_start(
-                    out=out_all[:, :, a, half * 512 : (half + 1) * 512],
-                    in_=oh[:, a, :].unsqueeze(1).to_broadcast([P, R, 512]),
-                )
-
         def l1_tile(c, al, tag):
             bank = psum.tile([P, 4, P], F32, name="acc1t", tag=tag)
             for j in range(4):
@@ -249,6 +243,36 @@ def tile_multilayerallreduce_pa_t_kernel(tc, x, w_first, w_second, out):
                     for g in range(2):
                         l1_pass(bank[:, j, :], j, r, g, xq[c][0], xq[c][1], g * 256 + al * P, P)
             return bank
+
+        def l1_pair(c, tags):
+            banks = []
+            for b in range(2):
+                bank = psum.tile([P, 2, 256], F32, name="acc1p", tag=tags[b])
+                for jj in range(2):
+                    for r in range(R):
+                        for g in range(2):
+                            l1_pass(bank[:, jj, :], 2 * b + jj, r, g, xq[c][0], xq[c][1], g * 256, 256)
+                banks.append(bank)
+            return banks
+
+        def red_pair(banks):
+            rgp = red.tile([P, 4 * 256], BF16, name="rgp", tag="rgp", align_bytes=64)
+            view = rgp[:].rearrange("p (m j) -> p m j", j=4)
+            nc.scalar.copy(out=view[:, :, 0:2], in_=banks[0][:].rearrange("p j m -> p m j"))
+            nc.vector.tensor_copy(out=view[:, :, 2:4], in_=banks[1][:].rearrange("p j m -> p m j"))
+            rcp = red.tile([P, 256], U32, name="rcp", tag="rcp", align_bytes=64)
+            rsp = red.tile([P, 256], U8, name="rsp", tag="rsp", align_bytes=64)
+            return rgp, rcp, rsp
+
+        def red_pair_quantise(t):
+            nc.vector.quantize_mx(out=t[1][:].bitcast(FP8X4), scales=t[2][:], in_=t[0][:])
+
+        def l2_tile_of(rc, rs, lo, ot, al, tags, engines):
+            for hh in range(2):
+                acc = psum.tile([P, 512], F32, name="acc2t", tag=tags[hh])
+                for r in range(R):
+                    l2_pass(acc[:], rc, rs, lo, hh, r)
+                copy_on(engines[hh], ot[:, al, hh * 512 : (hh + 1) * 512], acc[:])
 
         def red_tile(bank):
             rgt = red.tile([P, 4 * P], BF16, name="rgt", tag="rgt", align_bytes=64)
@@ -290,12 +314,6 @@ def tile_multilayerallreduce_pa_t_kernel(tc, x, w_first, w_second, out):
             for a in tiles:
                 l2_pass(accs[a][:], rq0s[a][0], rq0s[a][1], 0, half, rr)
 
-        def out_half(accs, oh, half, engines):
-            for a in range(4):
-                copy_on(engines[a], oh[:, a, :], accs[a][:])
-                if a % 2 == 1:
-                    store_half(oh, half, a - 1, 2)
-
         g0 = w_regroup(w2r[0], VG2)
         g1 = w_regroup(w2r[1], VG2)
         q2(0, g0)
@@ -319,60 +337,84 @@ def tile_multilayerallreduce_pa_t_kernel(tc, x, w_first, w_second, out):
         l2_tiles(h0, (0, 1, 2, 3), 0, 3)
         xb0 = x_transpose(xr1[0], 0, 2, ["b4", "b5"])
         xb1 = x_transpose(xr1[1], 0, 2, ["b6", "b7"])
+        def store_tile_half(ot, al, a, half):
+            nc.sync.dma_start(
+                out=out_all[:, :, a, half * 512 : (half + 1) * 512],
+                in_=ot[:, al, half * 512 : (half + 1) * 512].unsqueeze(1).to_broadcast([P, R, 512]),
+            )
+
+        def store_tokens(ot, al, n, a):
+            nc.sync.dma_start(
+                out=out_flat[:, :, a * H : (a + n) * H],
+                in_=ot[:, al : al + n, :].rearrange("p a n -> p (a n)").unsqueeze(1).to_broadcast([P, R, n * H]),
+            )
+
         g4 = w_regroup(w2r[4], VG3)
         g5 = w_regroup(w2r[5], VG3)
         q2(4, g4)
-        oh0 = big.tile([P, 4, 512], F32, name="oh0", tag="big")
-        out_half(h0, oh0, 0, H0_ENG)
+        ot0 = big.tile([P, 2, H], F32, name="ot", tag="big")
+        ot1 = big.tile([P, 2, H], F32, name="ot", tag="big")
+        copy_on("s", ot0[:, 0, 0:512], h0[0][:])
+        store_tile_half(ot0, 0, 0, 0)
+        copy_on("v", ot0[:, 1, 0:512], h0[1][:])
+        store_tile_half(ot0, 1, 1, 0)
+        copy_on("s", ot1[:, 0, 0:512], h0[2][:])
+        copy_on("v", ot1[:, 1, 0:512], h0[3][:])
         g6 = w_regroup(w2r[6], VG3)
         q2(5, g5)
         xg0 = x_group(xb0, "ss")
         g7 = w_regroup(w2r[7], VG3)
         q2(6, g6)
         xg1 = x_group(xb1, "ss")
-        xq_(0, 0, xg0)
         q2(7, g7)
+        xq_(0, 0, xg0)
         xq_(0, 1, xg1)
         h1 = open_banks(B03)
         for rr in range(2):
             l2_tiles(h1, (0, 1, 2, 3), 1, rr)
+        for rr in range(2, 4):
+            l2_tiles(h1, (0, 1), 1, rr)
         xb2 = x_transpose(xr1[2], 0, 2, ["b4", "b5"])
         xb3 = x_transpose(xr1[3], 0, 2, ["b6", "b7"])
         for rr in range(2, 4):
-            l2_tiles(h1, (0, 1, 2, 3), 1, rr)
+            l2_tiles(h1, (2, 3), 1, rr)
+        copy_on("s", ot0[:, 0, 512:1024], h1[0][:])
+        store_tile_half(ot0, 0, 0, 1)
+        copy_on("v", ot0[:, 1, 512:1024], h1[1][:])
+        store_tile_half(ot0, 1, 1, 1)
         xg2 = x_group(xb2, "ss")
         xg3 = x_group(xb3, "sv")
         xq_(0, 2, xg2)
         xq_(0, 3, xg3)
-        oh1 = big.tile([P, 4, 512], F32, name="oh1", tag="big")
-        out_half(h1, oh1, 1, H1_ENG)
+        copy_on("s", ot1[:, 0, 512:1024], h1[2][:])
+        copy_on("v", ot1[:, 1, 512:1024], h1[3][:])
+        store_tokens(ot1, 0, 2, 2)
         xb0 = x_transpose(xr1[0], 2, 2, ["b6", "b7"])
-        bank0 = l1_tile(0, 0, "b4")
-        bank1 = l1_tile(0, 1, "b5")
+        pb = l1_pair(0, ["b4", "b5"])
         xb1 = x_transpose(xr1[1], 2, 2, ["b0", "b1"])
         xb2 = x_transpose(xr1[2], 2, 2, ["b2", "b3"])
         xg0 = x_group(xb0, "sv")
-        rq0 = red_tile(bank0)
+        rp = red_pair(pb)
         xq_(1, 0, xg0)
+        red_pair_quantise(rp)
         xg1 = x_group(xb1, "sv")
-        rq1 = red_tile(bank1)
         xq_(1, 1, xg1)
         xg2 = x_group(xb2, "sv")
         xb3 = x_transpose(xr1[3], 2, 2, ["b6", "b7"])
         xq_(1, 2, xg2)
         xg3 = x_group(xb3, "sv")
         ot = big.tile([P, 2, H], F32, name="ot", tag="big")
-        l2_tile(rq0, ot, 0, ["b4", "b5"], "sv")
-        nc.sync.dma_start(out=out_all[:, :, 4, :], in_=ot[:, 0, :].unsqueeze(1).to_broadcast([P, R, H]))
+        l2_tile_of(rp[1], rp[2], 0, ot, 0, ["b4", "b5"], "sv")
+        store_tokens(ot, 0, 1, 4)
         xq_(1, 3, xg3)
-        l2_tile(rq1, ot, 1, ["b0", "b1"], "sv")
-        nc.sync.dma_start(out=out_all[:, :, 5, :], in_=ot[:, 1, :].unsqueeze(1).to_broadcast([P, R, H]))
+        l2_tile_of(rp[1], rp[2], P, ot, 1, ["b0", "b1"], "sv")
+        store_tokens(ot, 1, 1, 5)
         bank0 = l1_tile(1, 0, "b2")
         rq0 = red_tile(bank0)
         bank1 = l1_tile(1, 1, "b3")
         rq1 = red_tile(bank1)
         ot = big.tile([P, 2, H], F32, name="ot", tag="big")
         l2_tile(rq0, ot, 0, ["b4", "b5"], "sv")
-        nc.sync.dma_start(out=out_all[:, :, 6, :], in_=ot[:, 0, :].unsqueeze(1).to_broadcast([P, R, H]))
+        store_tokens(ot, 0, 1, 6)
         l2_tile(rq1, ot, 1, ["b6", "b7"], "sv")
-        nc.sync.dma_start(out=out_all[:, :, 7, :], in_=ot[:, 1, :].unsqueeze(1).to_broadcast([P, R, H]))
+        store_tokens(ot, 1, 1, 7)

@@ -409,12 +409,21 @@ def tile_multilayerallreduce_pa_t_kernel(tc, x, w_first, w_second, out):
         xq_(1, 3, xg3)
         l2_tile_of(rp[1], rp[2], P, ot, 1, ["b0", "b1"], "sv")
         store_tokens(ot, 1, 1, 5)
-        bank0 = l1_tile(1, 0, "b2")
+        def l1_part(bank, al, js):
+            for j in js:
+                for r in range(R):
+                    for g in range(2):
+                        l1_pass(bank[:, j, :], j, r, g, xq[1][0], xq[1][1], g * 256 + al * P, P)
+
+        bank0 = psum.tile([P, 4, P], F32, name="acc1t", tag="b2")
+        bank1 = psum.tile([P, 4, P], F32, name="acc1t", tag="b3")
+        l1_part(bank0, 0, (0, 1, 2, 3))
         rq0 = red_tile(bank0)
-        bank1 = l1_tile(1, 1, "b3")
-        rq1 = red_tile(bank1)
+        l1_part(bank1, 1, (0, 1, 2))
         ot = big.tile([P, 2, H], F32, name="ot", tag="big")
         l2_tile(rq0, ot, 0, ["b4", "b5"], "sv")
         store_tokens(ot, 0, 1, 6)
+        l1_part(bank1, 1, (3,))
+        rq1 = red_tile(bank1)
         l2_tile(rq1, ot, 1, ["b6", "b7"], "sv")
         store_tokens(ot, 1, 1, 7)

@@ -123,10 +123,10 @@ def tile_multilayerallreduce_pa_t_kernel(tc, x, w_first, w_second, out):
 
         def w1_regroup(src, vec_cols):
             grouped = wgp.tile([P, 4 * 512], BF16, name="wg", tag="wg", align_bytes=64)
-            dv = grouped[:].rearrange("p (j m t) -> p j m t", j=4, t=4)
-            sv = src.rearrange("p t (m j) -> p j m t", j=4)
-            nc.vector.tensor_copy(out=dv[:, :, 0:vec_cols, :], in_=sv[:, :, 0:vec_cols, :])
-            nc.scalar.copy(out=dv[:, :, vec_cols:P, :], in_=sv[:, :, vec_cols:P, :])
+            dv = grouped[:].rearrange("p (j m t) -> p m t j", j=4, t=4)
+            sv = src.rearrange("p t (m j) -> p m t j", j=4)
+            nc.vector.tensor_copy(out=dv[:, 0:vec_cols, :, :], in_=sv[:, 0:vec_cols, :, :])
+            nc.scalar.copy(out=dv[:, vec_cols:P, :, :], in_=sv[:, vec_cols:P, :, :])
             return grouped
 
         def w_quantise(grouped, codes, scales):

from contextlib import ExitStack

import concourse.mybir as mybir
from concourse.masks import make_identity

FP8X4 = mybir.dt.float8_e4m3fn_x4
BF16 = mybir.dt.bfloat16
F32 = mybir.dt.float32
U32 = mybir.dt.uint32
U8 = mybir.dt.uint8

P = 128
R, T, H, F = 4, 1024, 1024, 512
A = T // P
FLOPS = 2 * R * T * H * F * 2

B03 = ["b0", "b1", "b2", "b3"]
B47 = ["b4", "b5", "b6", "b7"]
VG0 = 64
VG1 = 64
X1_ENG = "vsss"
VG2 = 80
VG3 = 80
RB_ENG = "ssvv"
H0_ENG = "svsv"
H1_ENG = "svsv"


def tile_multilayerallreduce_pa_t_kernel(tc, x, w_first, w_second, out):
    nc = tc.nc
    with ExitStack() as ctx:
        ctx.enter_context(tc.manual_schedule())
        const = ctx.enter_context(tc.tile_pool(name="const", bufs=1))
        xraw = ctx.enter_context(tc.tile_pool(name="xraw", bufs=4))
        big = ctx.enter_context(tc.tile_pool(name="big", bufs=8))
        xgp = ctx.enter_context(tc.tile_pool(name="xgp", bufs=2))
        wgp = ctx.enter_context(tc.tile_pool(name="wgp", bufs=3))
        keep = ctx.enter_context(tc.tile_pool(name="keep", bufs=1))
        red = ctx.enter_context(tc.tile_pool(name="red", bufs=2))
        psum = ctx.enter_context(tc.psum_pool(name="psum", bufs=1))

        x_flat = [x[r].rearrange("(m a) h -> m (a h)", a=A) for r in range(R)]
        out_all = out.rearrange("r (m a) n -> m r a n", a=A)
        out_flat = out.rearrange("r (m a) n -> m r (a n)", a=A)
        w1_view = [w_first[r].rearrange("(s p e) f -> p s (e f)", p=P, e=2) for r in range(R)]
        w2_view = [w_second[r].rearrange("(p j) n -> p j n", j=4) for r in range(R)]

        xr0 = []
        w1r = []
        for r in range(R):
            t0 = xraw.tile([P, 4 * H], BF16, name="xr0_%d" % r, tag="xr")
            xr0.append(t0)
            t1 = big.tile([P, 4, 2 * F], BF16, name="w1r_%d" % r, tag="big")
            w1r.append(t1)

        def load_x0(r, lo, n):
            nc.sync.dma_start(out=xr0[r][:, lo * H : (lo + n) * H], in_=x_flat[r][:, lo * H : (lo + n) * H])

        def load_w1(r, lo, n):
            nc.sync.dma_start(out=w1r[r][:, lo : lo + n, :], in_=w1_view[r][:, lo : lo + n, :])

        load_w1(0, 0, 2)
        load_x0(0, 0, 2)
        load_w1(0, 2, 2)
        load_x0(0, 2, 2)
        for r in range(1, R):
            load_x0(r, 0, 4)
            load_w1(r, 0, 4)
        units = [(half, r) for half in range(2) for r in range(R)]
        w2full = []
        for r in range(R):
            t2 = big.tile([P, 4, H], BF16, name="w2r_%d" % r, tag="big")
            nc.sync.dma_start(out=t2[:], in_=w2_view[r])
            w2full.append(t2)
        w2r = [w2full[r][:, :, half * 512 : (half + 1) * 512] for half, r in units]

        ident = const.tile([P, P], F32, name="ident")
        make_identity(nc, ident[:])

        w1c = keep.tile([P, 2 * R, F], U32, name="w1c", align_bytes=64)
        w1s = keep.tile([P, 2 * R, F], U8, name="w1s", align_bytes=64)
        w2c = keep.tile([P, R, H], U32, name="w2c", align_bytes=64)
        w2s = keep.tile([P, R, H], U8, name="w2s", align_bytes=64)

        def copy_on(engine, dst, src):
            if engine == "v":
                nc.vector.tensor_copy(out=dst, in_=src)
            else:
                nc.scalar.copy(out=dst, in_=src)

        def x_transpose(raw, a_lo, na, tags):
            words = raw[:].bitcast(F32)
            banks = []
            for a in range(na):
                bank = psum.tile([P, 4, P], F32, name="xt", tag=tags[a])
                for s in range(4):
                    lo = (a_lo + a) * (H // 2) + s * P
                    nc.tensor.transpose(bank[:, s, :], words[:, lo : lo + P], ident[:])
                banks.append(bank)
            return banks

        def x_group(banks, engines):
            na = len(banks)
            grouped = xgp.tile([P, 2 * na * P * 4], BF16, name="xg", tag="xg", align_bytes=64)
            gview = grouped[:].bitcast(F32).rearrange("p (g a m u) -> p g a m u", g=2, a=na, u=2)
            for a in range(na):
                copy_on(engines[a], gview[:, :, a, :, :], banks[a][:].rearrange("p (g u) m -> p g m u", g=2))
            return grouped

        def x_turn(raw, a_lo, na, engines, tags):
            return x_group(x_transpose(raw, a_lo, na, tags), engines)

        def x_quantise(grouped, r, codes, scales):
            nc.vector.quantize_mx(out=codes[:, r, :].bitcast(FP8X4), scales=scales[:, r, :], in_=grouped[:])

        def w_regroup(src, vec_groups):
            grouped = wgp.tile([P, 4 * 512], BF16, name="wg", tag="wg", align_bytes=64)
            dv = grouped[:].rearrange("p (c i t) -> p c t i", i=4, t=4)
            sv = src.rearrange("p t (c i) -> p c t i", i=4)
            nc.vector.tensor_copy(out=dv[:, 0:vec_groups, :, :], in_=sv[:, 0:vec_groups, :, :])
            nc.scalar.copy(out=dv[:, vec_groups:P, :, :], in_=sv[:, vec_groups:P, :, :])
            return grouped

        def w1_regroup(src, vec_cols):
            grouped = wgp.tile([P, 4 * 512], BF16, name="wg", tag="wg", align_bytes=64)
            dv = grouped[:].rearrange("p (j m t) -> p m t j", j=4, t=4)
            sv = src.rearrange("p t (m j) -> p m t j", j=4)
            nc.vector.tensor_copy(out=dv[:, 0:vec_cols, :, :], in_=sv[:, 0:vec_cols, :, :])
            nc.scalar.copy(out=dv[:, vec_cols:P, :, :], in_=sv[:, vec_cols:P, :, :])
            return grouped

        def w_quantise(grouped, codes, scales):
            nc.vector.quantize_mx(out=codes.bitcast(FP8X4), scales=scales, in_=grouped[:])

        def l1_pass(acc, j, r, g, codes, scales, lo, n):
            nc.tensor.matmul_mx(
                out=acc,
                lhsT=w1c[:, 2 * r + g, j * P : (j + 1) * P].bitcast(FP8X4),
                lhsT_scale=w1s[:, 2 * r + g, j * P : (j + 1) * P],
                rhs=codes[:, r, lo : lo + n].bitcast(FP8X4),
                rhs_scale=scales[:, r, lo : lo + n],
                start=(r == 0 and g == 0),
                stop=(r == R - 1 and g == 1),
            )

        def l1_open_pass(acc, j, r, g, lo):
            nc.tensor.matmul_mx(
                out=acc,
                lhsT=w1c[:, 2 * r + g, j * P : (j + 1) * P].bitcast(FP8X4),
                lhsT_scale=w1s[:, 2 * r + g, j * P : (j + 1) * P],
                rhs=xc0[:, r, lo : lo + P].bitcast(FP8X4),
                rhs_scale=xs0[:, r, lo : lo + P],
                start=(r == 0 and g == 0 and j == 0),
                stop=(r == R - 1 and g == 1 and j == 3),
            )

        def l2_pass(acc, rc, rs, lo, half, r):
            nc.tensor.matmul_mx(
                out=acc,
                lhsT=rc[:, lo : lo + P].bitcast(FP8X4),
                lhsT_scale=rs[:, lo : lo + P],
                rhs=w2c[:, r, half * 512 : (half + 1) * 512].bitcast(FP8X4),
                rhs_scale=w2s[:, r, half * 512 : (half + 1) * 512],
                start=(r == 0),
                stop=(r == R - 1),
            )

        xc0 = keep.tile([P, R, 1024], U32, name="xc0", align_bytes=64)
        xs0 = keep.tile([P, R, 1024], U8, name="xs0", align_bytes=64)
        acc1 = []

        def w1_rows(r, g):
            return w1r[r][:].rearrange("p s (e f) -> p (s e) f", e=2)[:, 4 * g : 4 * g + 4, :]

        def q1(r, g, grouped):
            w_quantise(grouped, w1c[:, 2 * r + g, :], w1s[:, 2 * r + g, :])

        wg0 = w1_regroup(w1_rows(0, 0), VG0)
        xb = x_transpose(xr0[0], 0, 4, B03)
        xgrp = xgp.tile([P, 2 * 4 * P * 4], BF16, name="xg", tag="xg", align_bytes=64)
        gv = xgrp[:].bitcast(F32).rearrange("p (g a m u) -> p g a m u", g=2, a=4, u=2)

        def ev0(a, e):
            copy_on(e, gv[:, :, a, :, :], xb[a][:].rearrange("p (g u) m -> p g m u", g=2))

        ev0(0, "s")
        q1(0, 0, wg0)
        ev0(1, "v")
        wg1 = w1_regroup(w1_rows(0, 1), VG0)
        ev0(2, "s")
        ev0(3, "v")
        q1(0, 1, wg1)
        xg = xgrp
        for r in range(R):
            if r > 0:
                wg0 = w1_regroup(w1_rows(r, 0), VG1)
                wg1 = w1_regroup(w1_rows(r, 1), VG1)
            x_quantise(xg, r, xc0, xs0)
            if r > 0:
                q1(r, 0, wg0)
            if r + 1 < R:
                xg = x_turn(xr0[r + 1], 0, 4, X1_ENG, B03)
            if r > 0:
                q1(r, 1, wg1)
            if r == 0:
                for a in range(4):
                    acc_a = psum.tile([P, 4, P], F32, name="acc1_%d" % a, tag=B47[a])
                    acc1.append(acc_a)
            for g in range(2):
                for j in range(4):
                    for a in range(4):
                        l1_open_pass(acc1[a][:, j, :], j, r, g, g * 512 + a * P)

        xr1 = []
        for r in range(R):
            t3 = xraw.tile([P, 4 * H], BF16, name="xr1_%d" % r, tag="xr")
            xr1.append(t3)

        def load_x1(c):
            for r in range(R):
                nc.sync.dma_start(
                    out=xr1[r][:, 2 * c * H : (2 * c + 2) * H],
                    in_=x_flat[r][:, (4 + 2 * c) * H : (6 + 2 * c) * H],
                )

        for r in range(R):
            nc.sync.dma_start(out=xr1[r][:], in_=x_flat[r][:, 4 * H : 8 * H])

        xq = []
        for c in range(2):
            codes = keep.tile([P, R, 512], U32, name="xc_%d" % c, align_bytes=64)
            scales = keep.tile([P, R, 512], U8, name="xs_%d" % c, align_bytes=64)
            xq.append((codes, scales))

        def q2(u, grouped):
            half, r = units[u]
            w_quantise(grouped, w2c[:, r, half * 512 : (half + 1) * 512], w2s[:, r, half * 512 : (half + 1) * 512])

        def l1_tile(c, al, tag):
            bank = psum.tile([P, 4, P], F32, name="acc1t", tag=tag)
            for j in range(4):
                for r in range(R):
                    for g in range(2):
                        l1_pass(bank[:, j, :], j, r, g, xq[c][0], xq[c][1], g * 256 + al * P, P)
            return bank

        def l1_pair(c, tags):
            banks = []
            for b in range(2):
                bank = psum.tile([P, 2, 256], F32, name="acc1p", tag=tags[b])
                for jj in range(2):
                    for r in range(R):
                        for g in range(2):
                            l1_pass(bank[:, jj, :], 2 * b + jj, r, g, xq[c][0], xq[c][1], g * 256, 256)
                banks.append(bank)
            return banks

        def red_pair(banks):
            rgp = red.tile([P, 4 * 256], BF16, name="rgp", tag="rgp", align_bytes=64)
            view = rgp[:].rearrange("p (m j) -> p m j", j=4)
            nc.scalar.copy(out=view[:, :, 0:2], in_=banks[0][:].rearrange("p j m -> p m j"))
            nc.vector.tensor_copy(out=view[:, :, 2:4], in_=banks[1][:].rearrange("p j m -> p m j"))
            rcp = red.tile([P, 256], U32, name="rcp", tag="rcp", align_bytes=64)
            rsp = red.tile([P, 256], U8, name="rsp", tag="rsp", align_bytes=64)
            return rgp, rcp, rsp

        def red_pair_quantise(t):
            nc.vector.quantize_mx(out=t[1][:].bitcast(FP8X4), scales=t[2][:], in_=t[0][:])

        def l2_tile_of(rc, rs, lo, ot, al, tags, engines):
            for hh in range(2):
                acc = psum.tile([P, 512], F32, name="acc2t", tag=tags[hh])
                for r in range(R):
                    l2_pass(acc[:], rc, rs, lo, hh, r)
                copy_on(engines[hh], ot[:, al, hh * 512 : (hh + 1) * 512], acc[:])

        def red_tile(bank):
            rgt = red.tile([P, 4 * P], BF16, name="rgt", tag="rgt", align_bytes=64)
            nc.scalar.copy(out=rgt[:].rearrange("p (m j) -> p m j", j=4), in_=bank[:].rearrange("p j m -> p m j"))
            rct = red.tile([P, P], U32, name="rct", tag="rct", align_bytes=64)
            rst = red.tile([P, P], U8, name="rst", tag="rst", align_bytes=64)
            nc.vector.quantize_mx(out=rct[:].bitcast(FP8X4), scales=rst[:], in_=rgt[:])
            return rct, rst

        def l2_tile(rq, ot, al, tags, engines):
            for hh in range(2):
                acc = psum.tile([P, 512], F32, name="acc2t", tag=tags[hh])
                for r in range(R):
                    l2_pass(acc[:], rq[0], rq[1], 0, hh, r)
                copy_on(engines[hh], ot[:, al, hh * 512 : (hh + 1) * 512], acc[:])

        def xq_(c, r, grouped):
            x_quantise(grouped, r, xq[c][0], xq[c][1])

        def red0_copy(a):
            rgt = keep.tile([P, 4 * P], BF16, name="rg0_%d" % a, align_bytes=64)
            nc.scalar.copy(out=rgt[:].rearrange("p (m j) -> p m j", j=4), in_=acc1[a][:].rearrange("p j m -> p m j"))
            return rgt

        def red0_quantise(a, rgt):
            rct = keep.tile([P, P], U32, name="rc0_%d" % a, align_bytes=64)
            rst = keep.tile([P, P], U8, name="rs0_%d" % a, align_bytes=64)
            nc.vector.quantize_mx(out=rct[:].bitcast(FP8X4), scales=rst[:], in_=rgt[:])
            return rct, rst

        def open_banks(tags):
            accs = []
            for i in range(len(tags)):
                acc_i = psum.tile([P, 512], F32, name="acc2", tag=tags[i])
                accs.append(acc_i)
            return accs

        def l2_tiles(accs, tiles, half, rr):
            for a in tiles:
                l2_pass(accs[a][:], rq0s[a][0], rq0s[a][1], 0, half, rr)

        g0 = w_regroup(w2r[0], VG2)
        g1 = w_regroup(w2r[1], VG2)
        q2(0, g0)
        rgs = [red0_copy(a) for a in range(4)]
        rq0s = []
        q2(1, g1)
        rq0s.append(red0_quantise(0, rgs[0]))
        rq0s.append(red0_quantise(1, rgs[1]))
        g2 = w_regroup(w2r[2], VG2)
        rq0s.append(red0_quantise(2, rgs[2]))
        rq0s.append(red0_quantise(3, rgs[3]))
        g3 = w_regroup(w2r[3], VG2)
        q2(2, g2)
        q2(3, g3)
        h0 = open_banks(B03)
        l2_tiles(h0, (0, 1), 0, 0)
        l2_tiles(h0, (0, 1), 0, 1)
        l2_tiles(h0, (2, 3), 0, 0)
        l2_tiles(h0, (2, 3), 0, 1)
        l2_tiles(h0, (0, 1, 2, 3), 0, 2)
        l2_tiles(h0, (0, 1, 2, 3), 0, 3)
        xb0 = x_transpose(xr1[0], 0, 2, ["b4", "b5"])
        xb1 = x_transpose(xr1[1], 0, 2, ["b6", "b7"])
        def store_tile_half(ot, al, a, half):
            nc.sync.dma_start(
                out=out_all[:, :, a, half * 512 : (half + 1) * 512],
                in_=ot[:, al, half * 512 : (half + 1) * 512].unsqueeze(1).to_broadcast([P, R, 512]),
            )

        def store_tokens(ot, al, n, a):
            nc.sync.dma_start(
                out=out_flat[:, :, a * H : (a + n) * H],
                in_=ot[:, al : al + n, :].rearrange("p a n -> p (a n)").unsqueeze(1).to_broadcast([P, R, n * H]),
            )

        g4 = w_regroup(w2r[4], VG3)
        g5 = w_regroup(w2r[5], VG3)
        q2(4, g4)
        ot0 = big.tile([P, 2, H], F32, name="ot", tag="big")
        ot1 = big.tile([P, 2, H], F32, name="ot", tag="big")
        copy_on("s", ot0[:, 0, 0:512], h0[0][:])
        store_tile_half(ot0, 0, 0, 0)
        copy_on("v", ot0[:, 1, 0:512], h0[1][:])
        store_tile_half(ot0, 1, 1, 0)
        copy_on("s", ot1[:, 0, 0:512], h0[2][:])
        copy_on("v", ot1[:, 1, 0:512], h0[3][:])
        g6 = w_regroup(w2r[6], VG3)
        q2(5, g5)
        xg0 = x_group(xb0, "ss")
        g7 = w_regroup(w2r[7], VG3)
        q2(6, g6)
        xg1 = x_group(xb1, "ss")
        q2(7, g7)
        xq_(0, 0, xg0)
        xq_(0, 1, xg1)
        h1 = open_banks(B03)
        for rr in range(2):
            l2_tiles(h1, (0, 1, 2, 3), 1, rr)
        for rr in range(2, 4):
            l2_tiles(h1, (0, 1), 1, rr)
        xb2 = x_transpose(xr1[2], 0, 2, ["b4", "b5"])
        xb3 = x_transpose(xr1[3], 0, 2, ["b6", "b7"])
        for rr in range(2, 4):
            l2_tiles(h1, (2, 3), 1, rr)
        copy_on("s", ot0[:, 0, 512:1024], h1[0][:])
        store_tile_half(ot0, 0, 0, 1)
        copy_on("v", ot0[:, 1, 512:1024], h1[1][:])
        store_tile_half(ot0, 1, 1, 1)
        xg2 = x_group(xb2, "ss")
        xg3 = x_group(xb3, "sv")
        xq_(0, 2, xg2)
        xq_(0, 3, xg3)
        copy_on("s", ot1[:, 0, 512:1024], h1[2][:])
        copy_on("v", ot1[:, 1, 512:1024], h1[3][:])
        store_tokens(ot1, 0, 2, 2)
        xb0 = x_transpose(xr1[0], 2, 2, ["b6", "b7"])
        pb = l1_pair(0, ["b4", "b5"])
        xb1 = x_transpose(xr1[1], 2, 2, ["b0", "b1"])
        xb2 = x_transpose(xr1[2], 2, 2, ["b2", "b3"])
        xg0 = x_group(xb0, "sv")
        rp = red_pair(pb)
        xq_(1, 0, xg0)
        red_pair_quantise(rp)
        xg1 = x_group(xb1, "sv")
        xq_(1, 1, xg1)
        xg2 = x_group(xb2, "sv")
        xb3 = x_transpose(xr1[3], 2, 2, ["b6", "b7"])
        xq_(1, 2, xg2)
        xg3 = x_group(xb3, "sv")
        ot = big.tile([P, 2, H], F32, name="ot", tag="big")
        l2_tile_of(rp[1], rp[2], 0, ot, 0, ["b4", "b5"], "sv")
        store_tokens(ot, 0, 1, 4)
        xq_(1, 3, xg3)
        l2_tile_of(rp[1], rp[2], P, ot, 1, ["b0", "b1"], "sv")
        store_tokens(ot, 1, 1, 5)
        def l1_part(bank, al, js):
            for j in js:
                for r in range(R):
                    for g in range(2):
                        l1_pass(bank[:, j, :], j, r, g, xq[1][0], xq[1][1], g * 256 + al * P, P)

        bank0 = psum.tile([P, 4, P], F32, name="acc1t", tag="b2")
        bank1 = psum.tile([P, 4, P], F32, name="acc1t", tag="b3")
        l1_part(bank0, 0, (0, 1, 2, 3))
        rq0 = red_tile(bank0)
        l1_part(bank1, 1, (0, 1, 2))
        ot = big.tile([P, 2, H], F32, name="ot", tag="big")
        l2_tile(rq0, ot, 0, ["b4", "b5"], "sv")
        store_tokens(ot, 0, 1, 6)
        l1_part(bank1, 1, (3,))
        rq1 = red_tile(bank1)
        l2_tile(rq1, ot, 1, ["b6", "b7"], "sv")
        store_tokens(ot, 1, 1, 7)
